import numpy as np
import ml_dtypes


def mxq(x, axis, fmt="e4m3"):
    dtype, down = {"e4m3": (ml_dtypes.float8_e4m3fn, 7), "e5m2": (ml_dtypes.float8_e5m2, 14)}[fmt]
    v = np.moveaxis(np.asarray(x, np.float32).astype(ml_dtypes.bfloat16).astype(np.float64), axis, -1)
    blocks = v.reshape(v.shape[:-1] + (-1, 32))
    amax = np.abs(blocks).max(-1, keepdims=True)
    byte = np.maximum(np.where(amax > 0, np.frexp(amax)[1] - 1 + 127, 0) - down, 1)
    scale = np.exp2(byte - 127.0)
    codes = (blocks / scale).astype(np.float32).astype(dtype).astype(np.float64)
    return np.moveaxis((codes * scale).reshape(v.shape), -1, axis)


WIDE = False


def mx_kscale(k):
    if not WIDE:
        return np.ones(k)
    levels = np.array([10, -10, 5, -5, 0])
    a = np.random.permutation(np.resize(levels, k // 512 * 4)).reshape(k // 512, 4)
    idx = np.arange(k)
    return np.exp2(a[idx // 512, idx % 128 // 32])


BF16 = ml_dtypes.bfloat16


def bf(x):
    return np.asarray(x, np.float32).astype(BF16)


def f64(x):
    return np.asarray(x).astype(np.float64)


B, C_IN, C_OUT, N, T, K = 1, 512, 128, 1024, 3, 3


def cheb_laplacian(p):
    adj = 1.0 / (1.0 + np.exp(-p))
    adj = (adj + adj.T) * 0.5
    adj = adj * (1.0 - np.eye(N))
    deg = adj.sum(axis=1)
    dis = 1.0 / np.sqrt(deg)
    return -(dis[:, None] * adj * dis[None, :])


def setup_inputs():
    s = mx_kscale(C_IN)
    x = np.random.standard_normal((B, C_IN, 1, T)) + np.random.standard_normal((B, C_IN, N, T))
    return {'x': bf(x * s[None, :, None, None]),
            'adj_param': bf(4.0 * np.random.standard_normal((N, N)) - 10.0 + 10.0 * np.eye(N)),
            'w_cheb0': bf(np.random.standard_normal((C_IN, C_OUT)) / np.sqrt(C_IN) / s[:, None]),
            'w_cheb1': bf(np.random.standard_normal((C_IN, C_OUT)) / np.sqrt(C_IN) / s[:, None])}


def reference(x, adj_param, w_cheb0, w_cheb1):
    s = cheb_laplacian(f64(adj_param))
    xt = f64(x).transpose(0, 3, 2, 1)
    h = mxq(xt, 3, 'e4m3') @ mxq(f64(w_cheb0), 0, 'e4m3')
    tx1 = mxq(s, 1, 'e4m3') @ mxq(xt, 2, 'e4m3')
    h = h + (mxq(tx1, 3, 'e4m3') @ mxq(f64(w_cheb1), 0, 'e4m3'))
    return h

@@ -1,0 +1,297 @@
+from contextlib import ExitStack
+
+import concourse.mybir as mybir
+from concourse.masks import make_identity
+
+F32 = mybir.dt.float32
+BF16 = mybir.dt.bfloat16
+U32 = mybir.dt.uint32
+U8 = mybir.dt.uint8
+FP8X4 = mybir.dt.float8_e4m3fn_x4
+ACT = mybir.ActivationFunctionType
+ALU = mybir.AluOpType
+
+P = 128
+PACK = 4
+NODES = 1024
+C_IN = 512
+C_OUT = 128
+T = 3
+QUARTERS = 4
+QUARTER = NODES // QUARTERS
+SLOTS = 8
+HALF = NODES // 2
+
+FLOPS = 2 * NODES * NODES * T * C_IN + 2 * 2 * T * NODES * C_IN * C_OUT
+
+
+def tile_dynamicgraphspatialconv_pa_kernel(tc, x, adj_param, w_cheb0, w_cheb1, out):
+    nc = tc.nc
+    with ExitStack() as stack:
+        keep = stack.enter_context(tc.tile_pool(name="keep", bufs=1))
+        xd_pool = stack.enter_context(tc.tile_pool(name="xd_pool", bufs=4))
+        stage = stack.enter_context(tc.tile_pool(name="stage", bufs=2))
+        psum = stack.enter_context(tc.psum_pool(name="psum", bufs=4))
+
+        ident = keep.tile([P, P], F32)
+        make_identity(nc, ident[:])
+
+        adj_rows = adj_param.rearrange("(h q e) m -> h q (e m)", h=QUARTERS, e=2)
+        x_rows = x[0].rearrange("(p j) (h n) t -> h p j (n t)", j=PACK, h=QUARTERS)
+        adj_sb = [keep.tile([P, 2, NODES], BF16, name="adj%d" % h) for h in range(QUARTERS)]
+        x_raw = [keep.tile([P, PACK, QUARTER * T], BF16, name="xraw%d" % h) for h in range(QUARTERS)]
+
+        def load_adj(h):
+            nc.sync.dma_start(out=adj_sb[h][:].rearrange("q e m -> q (e m)"), in_=adj_rows[h])
+
+        def load_x(h):
+            nc.sync.dma_start(out=x_raw[h][:], in_=x_rows[h])
+
+        load_adj(0)
+        load_x(0)
+        load_adj(1)
+        load_adj(2)
+        load_x(1)
+        load_adj(3)
+        load_x(2)
+        load_x(3)
+        w_raw = keep.tile([P, 2, PACK, C_OUT], BF16)
+        nc.scalar.dma_start(out=w_raw[:, 0], in_=w_cheb0.rearrange("(p j) o -> p j o", j=PACK))
+        nc.scalar.dma_start(out=w_raw[:, 1], in_=w_cheb1.rearrange("(p j) o -> p j o", j=PACK))
+
+        w_grouped = keep.tile([P, 2, C_OUT, PACK], BF16, align_bytes=64)
+        w_codes = keep.tile([P, 2, C_OUT], U32, align_bytes=64)
+        w_scales = keep.tile([P, 2, C_OUT], U8, align_bytes=64)
+        nc.vector.tensor_copy(out=w_grouped[:], in_=w_raw[:].rearrange("p k j o -> p k o j"))
+        nc.vector.quantize_mx(
+            out=w_codes[:].rearrange("p k o -> p (k o)").bitcast(FP8X4),
+            scales=w_scales[:].rearrange("p k o -> p (k o)"),
+            in_=w_grouped[:].rearrange("p k o j -> p (k o j)"),
+        )
+
+        sig = keep.tile([P, SLOTS, NODES], F32)
+        sym = keep.tile([P, SLOTS, NODES], F32)
+        deg_parts = keep.tile([P, SLOTS, 2], F32)
+
+        def sigmoid(slot, half):
+            cols = slice(half * HALF, (half + 1) * HALF)
+            nc.scalar.activation(
+                out=sig[:, slot, cols].rearrange("q (hc ec qc) -> q hc ec qc", hc=2, ec=2),
+                in_=adj_sb[slot // 2][:, slot % 2, cols].rearrange("q (hc qc ec) -> q hc ec qc", hc=2, ec=2),
+                func=ACT.Sigmoid,
+            )
+            if slot // PACK == half:
+                diagonal_block = sig[:, slot, slot * P : (slot + 1) * P]
+                nc.gpsimd.affine_select(
+                    out=diagonal_block,
+                    in_=diagonal_block,
+                    pattern=[[-1, P]],
+                    compare_op=ALU.not_equal,
+                    fill=0.0,
+                    base=0,
+                    channel_multiplier=1,
+                )
+
+        def symmetrise(slot, half):
+            cols = slice(half * HALF, (half + 1) * HALF)
+            flipped = psum.tile([P, PACK, P], F32, tag="work")
+            for k in range(PACK):
+                nc.tensor.transpose(flipped[:, k, :], sig[:, half * PACK + k, slot * P : (slot + 1) * P], ident[:])
+            nc.vector.scalar_tensor_tensor(
+                out=sym[:, slot, cols],
+                in0=flipped[:].rearrange("q k w -> q (k w)"),
+                scalar=1.0,
+                in1=sig[:, slot, cols],
+                op0=ALU.mult,
+                op1=ALU.add,
+                accum_out=deg_parts[:, slot, half : half + 1],
+            )
+
+        xn_codes = keep.tile([P, 2, T, PACK, P], U32, align_bytes=64)
+        xn_scales = keep.tile([P, 2, T, PACK, P], U8, align_bytes=64)
+
+        by_time = [xd_pool.tile([P, PACK, T, QUARTER], BF16, name="x_t%d" % h, tag="x_t") for h in range(QUARTERS)]
+
+        def split_times(h):
+            if h < QUARTERS - 1:
+                for j in range(PACK):
+                    nc.gpsimd.tensor_scalar(
+                        out=by_time[h][:, j],
+                        in0=x_raw[h][:, j].rearrange("p (n t) -> p t n", t=T),
+                        scalar1=1.0,
+                        scalar2=0.0,
+                        op0=ALU.mult,
+                        op1=ALU.add,
+                    )
+            else:
+                nc.vector.tensor_copy(out=by_time[h][:], in_=x_raw[h][:].rearrange("p j (n t) -> p j t n", t=T))
+
+        def x_over_nodes(g):
+            for t in range(T):
+                xn_grouped = stage.tile([P, PACK, P, PACK], BF16, align_bytes=64)
+                for jp in range(2):
+                    pairs = psum.tile([P, 2, 2, P], F32, tag="work")
+                    for u in range(2):
+                        for jj in range(2):
+                            nc.tensor.transpose(
+                                pairs[:, u, jj, :], by_time[2 * g + u][:, 2 * jp + jj, t, :].bitcast(F32), ident[:]
+                            )
+                    nc.scalar.copy(
+                        out=xn_grouped[:, 2 * jp : 2 * jp + 2].bitcast(F32),
+                        in_=pairs[:].rearrange("q u jj p -> q jj p u"),
+                    )
+                nc.vector.quantize_mx(
+                    out=xn_codes[:, g, t].rearrange("q j p -> q (j p)").bitcast(FP8X4),
+                    scales=xn_scales[:, g, t].rearrange("q j p -> q (j p)"),
+                    in_=xn_grouped[:].rearrange("q j p v -> q (j p v)"),
+                )
+
+        for slot in range(PACK):
+            sigmoid(slot, 0)
+            sigmoid(slot, 1)
+        split_times(0)
+        for slot in range(PACK):
+            symmetrise(slot, 0)
+        for slot in range(PACK, SLOTS):
+            sigmoid(slot, 0)
+        split_times(1)
+        for slot in range(PACK):
+            symmetrise(slot, 1)
+            symmetrise(slot + PACK, 0)
+        for slot in range(PACK, SLOTS):
+            sigmoid(slot, 1)
+        warm = keep.tile([P, 1], F32)
+        nc.scalar.activation(out=warm[:], in_=sig[:, SLOTS - 1, NODES - 1 : NODES], func=ACT.Sqrt)
+        x_over_nodes(0)
+        for slot in range(PACK, SLOTS):
+            symmetrise(slot, 1)
+        split_times(2)
+        split_times(3)
+
+        deg = keep.tile([P, SLOTS], F32)
+        root = keep.tile([P, SLOTS], F32)
+        inv_root = keep.tile([P, SLOTS], F32)
+        neg_inv_root = keep.tile([P, SLOTS], F32)
+        nc.vector.tensor_tensor(out=deg[:], in0=deg_parts[:, :, 0], in1=deg_parts[:, :, 1], op=ALU.add)
+        nc.scalar.activation(out=root[:], in_=deg[:], func=ACT.Sqrt)
+        nc.vector.reciprocal(out=inv_root[:], in_=root[:])
+        nc.vector.tensor_scalar(out=neg_inv_root[:], in0=inv_root[:], scalar1=-1.0, scalar2=None, op0=ALU.mult)
+        along_free = []
+        for half in range(2):
+            spread = psum.tile([P, PACK, P], F32, name="spread%d" % half, bufs=1)
+            for k in range(PACK):
+                slot = half * PACK + k
+                nc.tensor.matmul(
+                    out=spread[:, k, :],
+                    lhsT=neg_inv_root[:, slot : slot + 1].to_broadcast([P, P]),
+                    rhs=ident[:],
+                    start=True,
+                    stop=True,
+                )
+            along_free.append(spread)
+
+        def scale_rows(half):
+            cols = slice(half * HALF, (half + 1) * HALF)
+            for slot in range(SLOTS):
+                nc.vector.tensor_scalar(
+                    out=sym[:, slot, cols],
+                    in0=sym[:, slot, cols],
+                    scalar1=inv_root[:, slot : slot + 1],
+                    scalar2=None,
+                    op0=ALU.mult,
+                )
+
+        scale_rows(0)
+        x_over_nodes(1)
+
+        xc_codes = keep.tile([P, T, NODES], U32, align_bytes=64)
+        xc_scales = keep.tile([P, T, NODES], U8, align_bytes=64)
+        for h in range(QUARTERS):
+            cols = slice(h * QUARTER, (h + 1) * QUARTER)
+            for t in range(T):
+                xc_grouped = stage.tile([P, 2, P, PACK], BF16, align_bytes=64, bufs=3)
+                nc.gpsimd.tensor_scalar(
+                    out=xc_grouped[:],
+                    in0=x_raw[h][:].rearrange("p j (q e t) -> p t e q j", e=2, t=T)[:, t],
+                    scalar1=1.0,
+                    scalar2=0.0,
+                    op0=ALU.mult,
+                    op1=ALU.add,
+                )
+                nc.vector.quantize_mx(
+                    out=xc_codes[:, t, cols].bitcast(FP8X4),
+                    scales=xc_scales[:, t, cols],
+                    in_=xc_grouped[:].rearrange("p e q j -> p (e q j)"),
+                )
+
+        s_codes = keep.tile([P, 2, NODES], U32, align_bytes=64)
+        s_scales = keep.tile([P, 2, NODES], U8, align_bytes=64)
+        tx_codes = keep.tile([P, T, NODES], U32, align_bytes=64)
+        tx_scales = keep.tile([P, T, NODES], U8, align_bytes=64)
+        out_rows = out[0].rearrange("t (h q e) o -> h e q t o", h=QUARTERS, e=2)
+        for h in range(QUARTERS):
+            cols = slice(h * QUARTER, (h + 1) * QUARTER)
+            if h == 2:
+                scale_rows(1)
+            s_grouped = stage.tile([P, 2, QUARTER, PACK], BF16, align_bytes=64)
+            for g in range(2):
+                nc.vector.tensor_tensor(
+                    out=s_grouped[:, g],
+                    in0=sym[:, g * PACK : (g + 1) * PACK, cols].rearrange("q v w -> q w v"),
+                    in1=along_free[h // 2][:, 2 * (h % 2) : 2 * (h % 2) + 2, :]
+                    .rearrange("q k w -> q (k w)")
+                    .unsqueeze(2)
+                    .to_broadcast([P, QUARTER, PACK]),
+                    op=ALU.mult,
+                )
+            for g in range(2):
+                nc.vector.quantize_mx(
+                    out=s_codes[:, g, cols].bitcast(FP8X4),
+                    scales=s_scales[:, g, cols],
+                    in_=s_grouped[:, g].rearrange("q w v -> q (w v)"),
+                )
+            for e in range(2):
+                block = slice((2 * h + e) * P, (2 * h + e + 1) * P)
+                tx_grouped = stage.tile([P, T, P, PACK], BF16, align_bytes=64, bufs=3)
+                for t in range(T):
+                    tx = psum.tile([P, PACK, P], F32, tag="work")
+                    for j in range(PACK):
+                        for g in range(2):
+                            nc.tensor.matmul_mx(
+                                out=tx[:, j, :],
+                                lhsT=xn_codes[:, g, t, j, :].bitcast(FP8X4),
+                                lhsT_scale=xn_scales[:, g, t, j, :],
+                                rhs=s_codes[:, g, block].bitcast(FP8X4),
+                                rhs_scale=s_scales[:, g, block],
+                                start=(g == 0),
+                                stop=(g == 1),
+                            )
+                    nc.scalar.copy(out=tx_grouped[:, t], in_=tx[:].rearrange("p j v -> p v j"))
+                    nc.vector.quantize_mx(
+                        out=tx_codes[:, t, block].bitcast(FP8X4),
+                        scales=tx_scales[:, t, block],
+                        in_=tx_grouped[:, t].rearrange("p v j -> p (v j)"),
+                    )
+                both = psum.tile([P, T, C_OUT], F32, tag="both", bufs=2)
+                for t in range(T):
+                    nc.tensor.matmul_mx(
+                        out=both[:, t, :],
+                        lhsT=xc_codes[:, t, block].bitcast(FP8X4),
+                        lhsT_scale=xc_scales[:, t, block],
+                        rhs=w_codes[:, 0, :].bitcast(FP8X4),
+                        rhs_scale=w_scales[:, 0, :],
+                        start=True,
+                        stop=False,
+                    )
+                    nc.tensor.matmul_mx(
+                        out=both[:, t, :],
+                        lhsT=tx_codes[:, t, block].bitcast(FP8X4),
+                        lhsT_scale=tx_scales[:, t, block],
+                        rhs=w_codes[:, 1, :].bitcast(FP8X4),
+                        rhs_scale=w_scales[:, 1, :],
+                        start=False,
+                        stop=True,
+                    )
+                result = stage.tile([P, T, C_OUT], F32, bufs=3)
+                nc.scalar.copy(out=result[:], in_=both[:])
+                nc.sync.dma_start(out=out_rows[h, e], in_=result[:])

@@ -113,18 +113,7 @@ def tile_dynamicgraphspatialconv_pa_kernel(tc, x, adj_param, w_cheb0, w_cheb1, o
         by_time = [xd_pool.tile([P, PACK, T, QUARTER], BF16, name="x_t%d" % h, tag="x_t") for h in range(QUARTERS)]
 
         def split_times(h):
-            if h < QUARTERS - 1:
-                for j in range(PACK):
-                    nc.gpsimd.tensor_scalar(
-                        out=by_time[h][:, j],
-                        in0=x_raw[h][:, j].rearrange("p (n t) -> p t n", t=T),
-                        scalar1=1.0,
-                        scalar2=0.0,
-                        op0=ALU.mult,
-                        op1=ALU.add,
-                    )
-            else:
-                nc.vector.tensor_copy(out=by_time[h][:], in_=x_raw[h][:].rearrange("p j (n t) -> p j t n", t=T))
+            nc.vector.tensor_copy(out=by_time[h][:], in_=x_raw[h][:].rearrange("p j (n t) -> p j t n", t=T))
 
         def x_over_nodes(g):
             for t in range(T):
@@ -210,13 +199,8 @@ def tile_dynamicgraphspatialconv_pa_kernel(tc, x, adj_param, w_cheb0, w_cheb1, o
             cols = slice(h * QUARTER, (h + 1) * QUARTER)
             for t in range(T):
                 xc_grouped = stage.tile([P, 2, P, PACK], BF16, align_bytes=64, bufs=3)
-                nc.gpsimd.tensor_scalar(
-                    out=xc_grouped[:],
-                    in0=x_raw[h][:].rearrange("p j (q e t) -> p t e q j", e=2, t=T)[:, t],
-                    scalar1=1.0,
-                    scalar2=0.0,
-                    op0=ALU.mult,
-                    op1=ALU.add,
+                nc.scalar.copy(
+                    out=xc_grouped[:], in_=x_raw[h][:].rearrange("p j (q e t) -> p t e q j", e=2, t=T)[:, t]
                 )
                 nc.vector.quantize_mx(
                     out=xc_codes[:, t, cols].bitcast(FP8X4),

@@ -17,10 +17,10 @@ NODES = 1024
 C_IN = 512
 C_OUT = 128
 T = 3
+SLOTS = NODES // P
+HALF = NODES // 2
 QUARTERS = 4
 QUARTER = NODES // QUARTERS
-SLOTS = 8
-HALF = NODES // 2
 
 FLOPS = 2 * NODES * NODES * T * C_IN + 2 * 2 * T * NODES * C_IN * C_OUT
 
@@ -29,20 +29,23 @@ def tile_dynamicgraphspatialconv_pa_kernel(tc, x, adj_param, w_cheb0, w_cheb1, o
     nc = tc.nc
     with ExitStack() as stack:
         keep = stack.enter_context(tc.tile_pool(name="keep", bufs=1))
-        xd_pool = stack.enter_context(tc.tile_pool(name="xd_pool", bufs=4))
         stage = stack.enter_context(tc.tile_pool(name="stage", bufs=2))
         psum = stack.enter_context(tc.psum_pool(name="psum", bufs=4))
 
         ident = keep.tile([P, P], F32)
         make_identity(nc, ident[:])
+        ident_bf = keep.tile([P, P], BF16)
+        make_identity(nc, ident_bf[:])
+        ones = keep.tile([P, 2], F32)
+        nc.vector.memset(ones[:], 1.0)
 
-        adj_rows = adj_param.rearrange("(h q e) m -> h q (e m)", h=QUARTERS, e=2)
+        adj_rows = adj_param.rearrange("(h s q) m -> h q s m", h=QUARTERS, q=P)
         x_rows = x[0].rearrange("(p j) (h n) t -> h p j (n t)", j=PACK, h=QUARTERS)
         adj_sb = [keep.tile([P, 2, NODES], BF16, name="adj%d" % h) for h in range(QUARTERS)]
         x_raw = [keep.tile([P, PACK, QUARTER * T], BF16, name="xraw%d" % h) for h in range(QUARTERS)]
 
         def load_adj(h):
-            nc.sync.dma_start(out=adj_sb[h][:].rearrange("q e m -> q (e m)"), in_=adj_rows[h])
+            nc.sync.dma_start(out=adj_sb[h][:], in_=adj_rows[h])
 
         def load_x(h):
             nc.sync.dma_start(out=x_raw[h][:], in_=x_rows[h])
@@ -59,27 +62,13 @@ def tile_dynamicgraphspatialconv_pa_kernel(tc, x, adj_param, w_cheb0, w_cheb1, o
         nc.scalar.dma_start(out=w_raw[:, 0], in_=w_cheb0.rearrange("(p j) o -> p j o", j=PACK))
         nc.scalar.dma_start(out=w_raw[:, 1], in_=w_cheb1.rearrange("(p j) o -> p j o", j=PACK))
 
-        w_grouped = keep.tile([P, 2, C_OUT, PACK], BF16, align_bytes=64)
-        w_codes = keep.tile([P, 2, C_OUT], U32, align_bytes=64)
-        w_scales = keep.tile([P, 2, C_OUT], U8, align_bytes=64)
-        nc.vector.tensor_copy(out=w_grouped[:], in_=w_raw[:].rearrange("p k j o -> p k o j"))
-        nc.vector.quantize_mx(
-            out=w_codes[:].rearrange("p k o -> p (k o)").bitcast(FP8X4),
-            scales=w_scales[:].rearrange("p k o -> p (k o)"),
-            in_=w_grouped[:].rearrange("p k o j -> p (k o j)"),
-        )
-
         sig = keep.tile([P, SLOTS, NODES], F32)
         sym = keep.tile([P, SLOTS, NODES], F32)
         deg_parts = keep.tile([P, SLOTS, 2], F32)
 
         def sigmoid(slot, half):
             cols = slice(half * HALF, (half + 1) * HALF)
-            nc.scalar.activation(
-                out=sig[:, slot, cols].rearrange("q (hc ec qc) -> q hc ec qc", hc=2, ec=2),
-                in_=adj_sb[slot // 2][:, slot % 2, cols].rearrange("q (hc qc ec) -> q hc ec qc", hc=2, ec=2),
-                func=ACT.Sigmoid,
-            )
+            nc.scalar.activation(out=sig[:, slot, cols], in_=adj_sb[slot // 2][:, slot % 2, cols], func=ACT.Sigmoid)
             if slot // PACK == half:
                 diagonal_block = sig[:, slot, slot * P : (slot + 1) * P]
                 nc.gpsimd.affine_select(
@@ -110,24 +99,19 @@ def tile_dynamicgraphspatialconv_pa_kernel(tc, x, adj_param, w_cheb0, w_cheb1, o
         xn_codes = keep.tile([P, 2, T, PACK, P], U32, align_bytes=64)
         xn_scales = keep.tile([P, 2, T, PACK, P], U8, align_bytes=64)
 
-        by_time = [xd_pool.tile([P, PACK, T, QUARTER], BF16, name="x_t%d" % h, tag="x_t") for h in range(QUARTERS)]
-
-        def split_times(h):
-            nc.vector.tensor_copy(out=by_time[h][:], in_=x_raw[h][:].rearrange("p j (n t) -> p j t n", t=T))
-
         def x_over_nodes(g):
             for t in range(T):
                 xn_grouped = stage.tile([P, PACK, P, PACK], BF16, align_bytes=64)
                 for jp in range(2):
-                    pairs = psum.tile([P, 2, 2, P], F32, tag="work")
-                    for u in range(2):
+                    flipped_x = psum.tile([P, PACK, 2, P], BF16, tag="work")
+                    for v in range(PACK):
+                        nodes_of_slot = x_raw[2 * g + v // 2][:].rearrange("p j (s q t) -> p j s t q", s=2, t=T)
                         for jj in range(2):
                             nc.tensor.transpose(
-                                pairs[:, u, jj, :], by_time[2 * g + u][:, 2 * jp + jj, t, :].bitcast(F32), ident[:]
+                                flipped_x[:, v, jj, :], nodes_of_slot[:, 2 * jp + jj, v % 2, t, :], ident_bf[:]
                             )
                     nc.scalar.copy(
-                        out=xn_grouped[:, 2 * jp : 2 * jp + 2].bitcast(F32),
-                        in_=pairs[:].rearrange("q u jj p -> q jj p u"),
+                        out=xn_grouped[:, 2 * jp : 2 * jp + 2], in_=flipped_x[:].rearrange("q v jj p -> q jj p v")
                     )
                 nc.vector.quantize_mx(
                     out=xn_codes[:, g, t].rearrange("q j p -> q (j p)").bitcast(FP8X4),
@@ -135,107 +119,126 @@ def tile_dynamicgraphspatialconv_pa_kernel(tc, x, adj_param, w_cheb0, w_cheb1, o
                     in_=xn_grouped[:].rearrange("q j p v -> q (j p v)"),
                 )
 
-        for slot in range(PACK):
-            sigmoid(slot, 0)
-            sigmoid(slot, 1)
-        split_times(0)
-        for slot in range(PACK):
-            symmetrise(slot, 0)
-        for slot in range(PACK, SLOTS):
-            sigmoid(slot, 0)
-        split_times(1)
-        for slot in range(PACK):
-            symmetrise(slot, 1)
-            symmetrise(slot + PACK, 0)
-        for slot in range(PACK, SLOTS):
-            sigmoid(slot, 1)
+        for h in range(QUARTERS):
+            for half in range(2):
+                sigmoid(2 * h, half)
+                sigmoid(2 * h + 1, half)
         warm = keep.tile([P, 1], F32)
         nc.scalar.activation(out=warm[:], in_=sig[:, SLOTS - 1, NODES - 1 : NODES], func=ACT.Sqrt)
+
+        for slot in range(PACK):
+            symmetrise(slot, 0)
         x_over_nodes(0)
+        for slot in range(PACK):
+            symmetrise(slot, 1)
+        mirror_sums = psum.tile([P, PACK, 2], F32, tag="both", bufs=2)
+        for k in range(PACK):
+            for slot in range(PACK):
+                nc.tensor.matmul(
+                    out=mirror_sums[:, k, :],
+                    lhsT=sym[:, slot, (PACK + k) * P : (PACK + k + 1) * P],
+                    rhs=ones[:],
+                    start=(slot == 0),
+                    stop=(slot == PACK - 1),
+                )
         for slot in range(PACK, SLOTS):
             symmetrise(slot, 1)
-        split_times(2)
-        split_times(3)
 
         deg = keep.tile([P, SLOTS], F32)
         root = keep.tile([P, SLOTS], F32)
         inv_root = keep.tile([P, SLOTS], F32)
         neg_inv_root = keep.tile([P, SLOTS], F32)
-        nc.vector.tensor_tensor(out=deg[:], in0=deg_parts[:, :, 0], in1=deg_parts[:, :, 1], op=ALU.add)
+        nc.vector.tensor_tensor(out=deg[:, :PACK], in0=deg_parts[:, :PACK, 0], in1=deg_parts[:, :PACK, 1], op=ALU.add)
+        nc.vector.tensor_tensor(out=deg[:, PACK:], in0=deg_parts[:, PACK:, 1], in1=mirror_sums[:, :, 0], op=ALU.add)
         nc.scalar.activation(out=root[:], in_=deg[:], func=ACT.Sqrt)
         nc.vector.reciprocal(out=inv_root[:], in_=root[:])
         nc.vector.tensor_scalar(out=neg_inv_root[:], in0=inv_root[:], scalar1=-1.0, scalar2=None, op0=ALU.mult)
-        along_free = []
-        for half in range(2):
-            spread = psum.tile([P, PACK, P], F32, name="spread%d" % half, bufs=1)
+        along_free = [psum.tile([P, PACK, P], F32, name="spread%d" % half, bufs=1) for half in range(2)]
+        for half in (1, 0):
             for k in range(PACK):
                 slot = half * PACK + k
                 nc.tensor.matmul(
-                    out=spread[:, k, :],
+                    out=along_free[half][:, k, :],
                     lhsT=neg_inv_root[:, slot : slot + 1].to_broadcast([P, P]),
                     rhs=ident[:],
                     start=True,
                     stop=True,
                 )
-            along_free.append(spread)
 
-        def scale_rows(half):
+        def scale_rows(slot, half):
             cols = slice(half * HALF, (half + 1) * HALF)
-            for slot in range(SLOTS):
-                nc.vector.tensor_scalar(
-                    out=sym[:, slot, cols],
-                    in0=sym[:, slot, cols],
-                    scalar1=inv_root[:, slot : slot + 1],
-                    scalar2=None,
-                    op0=ALU.mult,
-                )
+            nc.vector.tensor_scalar(
+                out=sym[:, slot, cols],
+                in0=sym[:, slot, cols],
+                scalar1=inv_root[:, slot : slot + 1],
+                scalar2=None,
+                op0=ALU.mult,
+            )
 
-        scale_rows(0)
+        for slot in range(SLOTS):
+            scale_rows(slot, 1)
         x_over_nodes(1)
+
+        w_grouped = keep.tile([P, 2, C_OUT, PACK], BF16, align_bytes=64)
+        w_codes = keep.tile([P, 2, C_OUT], U32, align_bytes=64)
+        w_scales = keep.tile([P, 2, C_OUT], U8, align_bytes=64)
+        nc.vector.tensor_copy(out=w_grouped[:], in_=w_raw[:].rearrange("p k j o -> p k o j"))
+        nc.vector.quantize_mx(
+            out=w_codes[:].rearrange("p k o -> p (k o)").bitcast(FP8X4),
+            scales=w_scales[:].rearrange("p k o -> p (k o)"),
+            in_=w_grouped[:].rearrange("p k o j -> p (k o j)"),
+        )
 
         xc_codes = keep.tile([P, T, NODES], U32, align_bytes=64)
         xc_scales = keep.tile([P, T, NODES], U8, align_bytes=64)
-        for h in range(QUARTERS):
-            cols = slice(h * QUARTER, (h + 1) * QUARTER)
-            for t in range(T):
-                xc_grouped = stage.tile([P, 2, P, PACK], BF16, align_bytes=64, bufs=3)
-                nc.scalar.copy(
-                    out=xc_grouped[:], in_=x_raw[h][:].rearrange("p j (q e t) -> p t e q j", e=2, t=T)[:, t]
-                )
-                nc.vector.quantize_mx(
-                    out=xc_codes[:, t, cols].bitcast(FP8X4),
-                    scales=xc_scales[:, t, cols],
-                    in_=xc_grouped[:].rearrange("p e q j -> p (e q j)"),
-                )
-
         s_codes = keep.tile([P, 2, NODES], U32, align_bytes=64)
         s_scales = keep.tile([P, 2, NODES], U8, align_bytes=64)
         tx_codes = keep.tile([P, T, NODES], U32, align_bytes=64)
         tx_scales = keep.tile([P, T, NODES], U8, align_bytes=64)
-        out_rows = out[0].rearrange("t (h q e) o -> h e q t o", h=QUARTERS, e=2)
-        for h in range(QUARTERS):
+        upper_right = keep.tile([P, HALF, PACK], BF16, align_bytes=64)
+        out_rows = out[0].rearrange("t (b q) o -> b q t o", q=P)
+
+        def scale_columns(g, h, grouped):
+            nc.vector.tensor_tensor(
+                out=grouped,
+                in0=sym[:, g * PACK : (g + 1) * PACK, h * QUARTER : (h + 1) * QUARTER].rearrange("q v w -> q w v"),
+                in1=along_free[h // 2][:, 2 * (h % 2) : 2 * (h % 2) + 2, :]
+                .rearrange("q k w -> q (k w)")
+                .unsqueeze(2)
+                .to_broadcast([P, QUARTER, PACK]),
+                op=ALU.mult,
+            )
+
+        def quantise_s(g, h, grouped):
             cols = slice(h * QUARTER, (h + 1) * QUARTER)
-            if h == 2:
-                scale_rows(1)
-            s_grouped = stage.tile([P, 2, QUARTER, PACK], BF16, align_bytes=64)
-            for g in range(2):
-                nc.vector.tensor_tensor(
-                    out=s_grouped[:, g],
-                    in0=sym[:, g * PACK : (g + 1) * PACK, cols].rearrange("q v w -> q w v"),
-                    in1=along_free[h // 2][:, 2 * (h % 2) : 2 * (h % 2) + 2, :]
-                    .rearrange("q k w -> q (k w)")
-                    .unsqueeze(2)
-                    .to_broadcast([P, QUARTER, PACK]),
-                    op=ALU.mult,
-                )
-            for g in range(2):
-                nc.vector.quantize_mx(
-                    out=s_codes[:, g, cols].bitcast(FP8X4),
-                    scales=s_scales[:, g, cols],
-                    in_=s_grouped[:, g].rearrange("q w v -> q (w v)"),
-                )
-            for e in range(2):
-                block = slice((2 * h + e) * P, (2 * h + e + 1) * P)
+            nc.vector.quantize_mx(
+                out=s_codes[:, g, cols].bitcast(FP8X4),
+                scales=s_scales[:, g, cols],
+                in_=grouped.rearrange("q w v -> q (w v)"),
+            )
+
+        for h in (2, 3, 0, 1):
+            lower = stage.tile([P, QUARTER, PACK], BF16, align_bytes=64)
+            if h >= 2:
+                upper = upper_right[:, (h - 2) * QUARTER : (h - 1) * QUARTER, :]
+                scale_columns(0, h, upper)
+                scale_columns(1, h, lower[:])
+            else:
+                if h == 0:
+                    for slot in range(PACK):
+                        scale_rows(slot, 0)
+                upper_left = stage.tile([P, QUARTER, PACK], BF16, align_bytes=64)
+                upper = upper_left[:]
+                scale_columns(0, h, upper)
+                for b in range(2):
+                    mirrored = psum.tile([P, PACK, P], BF16, tag="work")
+                    for k in range(PACK):
+                        nc.tensor.transpose(mirrored[:, k, :], upper_right[:, k * P : (k + 1) * P, 2 * h + b], ident_bf[:])
+                    nc.scalar.copy(out=lower[:, b * P : (b + 1) * P, :], in_=mirrored[:].rearrange("w k q -> w q k"))
+            quantise_s(0, h, upper)
+            quantise_s(1, h, lower[:])
+            for b in range(2):
+                block = slice((2 * h + b) * P, (2 * h + b + 1) * P)
                 tx_grouped = stage.tile([P, T, P, PACK], BF16, align_bytes=64, bufs=3)
                 for t in range(T):
                     tx = psum.tile([P, PACK, P], F32, tag="work")
@@ -256,6 +259,17 @@ def tile_dynamicgraphspatialconv_pa_kernel(tc, x, adj_param, w_cheb0, w_cheb1, o
                         scales=tx_scales[:, t, block],
                         in_=tx_grouped[:, t].rearrange("p v j -> p (v j)"),
                     )
+                if b == 0:
+                    for t in range(T):
+                        xc_grouped = stage.tile([P, QUARTER, PACK], BF16, align_bytes=64, bufs=3)
+                        nc.vector.tensor_copy(
+                            out=xc_grouped[:], in_=x_raw[h][:].rearrange("p j (n t) -> p t n j", t=T)[:, t]
+                        )
+                        nc.vector.quantize_mx(
+                            out=xc_codes[:, t, h * QUARTER : (h + 1) * QUARTER].bitcast(FP8X4),
+                            scales=xc_scales[:, t, h * QUARTER : (h + 1) * QUARTER],
+                            in_=xc_grouped[:].rearrange("p n j -> p (n j)"),
+                        )
                 both = psum.tile([P, T, C_OUT], F32, tag="both", bufs=2)
                 for t in range(T):
                     nc.tensor.matmul_mx(
@@ -278,4 +292,4 @@ def tile_dynamicgraphspatialconv_pa_kernel(tc, x, adj_param, w_cheb0, w_cheb1, o
                     )
                 result = stage.tile([P, T, C_OUT], F32, bufs=3)
                 nc.scalar.copy(out=result[:], in_=both[:])
-                nc.sync.dma_start(out=out_rows[h, e], in_=result[:])
+                nc.sync.dma_start(out=out_rows[2 * h + b], in_=result[:])

@@ -21,6 +21,7 @@ SLOTS = NODES // P
 HALF = NODES // 2
 QUARTERS = 4
 QUARTER = NODES // QUARTERS
+QUARTER_ORDER = (2, 3, 0, 1)
 
 FLOPS = 2 * NODES * NODES * T * C_IN + 2 * 2 * T * NODES * C_IN * C_OUT
 
@@ -43,21 +44,10 @@ def tile_dynamicgraphspatialconv_pa_kernel(tc, x, adj_param, w_cheb0, w_cheb1, o
         x_rows = x[0].rearrange("(p j) (h n) t -> h p j (n t)", j=PACK, h=QUARTERS)
         adj_sb = [keep.tile([P, 2, NODES], BF16, name="adj%d" % h) for h in range(QUARTERS)]
         x_raw = [keep.tile([P, PACK, QUARTER * T], BF16, name="xraw%d" % h) for h in range(QUARTERS)]
-
-        def load_adj(h):
+        for h in range(QUARTERS):
             nc.sync.dma_start(out=adj_sb[h][:], in_=adj_rows[h])
-
-        def load_x(h):
+        for h in QUARTER_ORDER:
             nc.sync.dma_start(out=x_raw[h][:], in_=x_rows[h])
-
-        load_adj(0)
-        load_x(0)
-        load_adj(1)
-        load_adj(2)
-        load_x(1)
-        load_adj(3)
-        load_x(2)
-        load_x(3)
         w_raw = keep.tile([P, 2, PACK, C_OUT], BF16)
         nc.scalar.dma_start(out=w_raw[:, 0], in_=w_cheb0.rearrange("(p j) o -> p j o", j=PACK))
         nc.scalar.dma_start(out=w_raw[:, 1], in_=w_cheb1.rearrange("(p j) o -> p j o", j=PACK))
@@ -83,7 +73,7 @@ def tile_dynamicgraphspatialconv_pa_kernel(tc, x, adj_param, w_cheb0, w_cheb1, o
 
         def symmetrise(slot, half):
             cols = slice(half * HALF, (half + 1) * HALF)
-            flipped = psum.tile([P, PACK, P], F32, tag="work")
+            flipped = psum.tile([P, PACK, P], F32, tag="a")
             for k in range(PACK):
                 nc.tensor.transpose(flipped[:, k, :], sig[:, half * PACK + k, slot * P : (slot + 1) * P], ident[:])
             nc.vector.scalar_tensor_tensor(
@@ -96,42 +86,16 @@ def tile_dynamicgraphspatialconv_pa_kernel(tc, x, adj_param, w_cheb0, w_cheb1, o
                 accum_out=deg_parts[:, slot, half : half + 1],
             )
 
-        xn_codes = keep.tile([P, 2, T, PACK, P], U32, align_bytes=64)
-        xn_scales = keep.tile([P, 2, T, PACK, P], U8, align_bytes=64)
-
-        def x_over_nodes(g):
-            for t in range(T):
-                xn_grouped = stage.tile([P, PACK, P, PACK], BF16, align_bytes=64)
-                for jp in range(2):
-                    flipped_x = psum.tile([P, PACK, 2, P], BF16, tag="work")
-                    for v in range(PACK):
-                        nodes_of_slot = x_raw[2 * g + v // 2][:].rearrange("p j (s q t) -> p j s t q", s=2, t=T)
-                        for jj in range(2):
-                            nc.tensor.transpose(
-                                flipped_x[:, v, jj, :], nodes_of_slot[:, 2 * jp + jj, v % 2, t, :], ident_bf[:]
-                            )
-                    nc.scalar.copy(
-                        out=xn_grouped[:, 2 * jp : 2 * jp + 2], in_=flipped_x[:].rearrange("q v jj p -> q jj p v")
-                    )
-                nc.vector.quantize_mx(
-                    out=xn_codes[:, g, t].rearrange("q j p -> q (j p)").bitcast(FP8X4),
-                    scales=xn_scales[:, g, t].rearrange("q j p -> q (j p)"),
-                    in_=xn_grouped[:].rearrange("q j p v -> q (j p v)"),
-                )
-
-        for h in range(QUARTERS):
-            for half in range(2):
-                sigmoid(2 * h, half)
-                sigmoid(2 * h + 1, half)
+        for half in range(2):
+            for slot in range(SLOTS):
+                sigmoid(slot, half)
         warm = keep.tile([P, 1], F32)
         nc.scalar.activation(out=warm[:], in_=sig[:, SLOTS - 1, NODES - 1 : NODES], func=ACT.Sqrt)
 
-        for slot in range(PACK):
-            symmetrise(slot, 0)
-        x_over_nodes(0)
-        for slot in range(PACK):
-            symmetrise(slot, 1)
-        mirror_sums = psum.tile([P, PACK, 2], F32, tag="both", bufs=2)
+        for half in range(2):
+            for slot in range(PACK):
+                symmetrise(slot, half)
+        mirror_sums = psum.tile([P, PACK, 2], F32, tag="b", bufs=3)
         for k in range(PACK):
             for slot in range(PACK):
                 nc.tensor.matmul(
@@ -153,17 +117,19 @@ def tile_dynamicgraphspatialconv_pa_kernel(tc, x, adj_param, w_cheb0, w_cheb1, o
         nc.scalar.activation(out=root[:], in_=deg[:], func=ACT.Sqrt)
         nc.vector.reciprocal(out=inv_root[:], in_=root[:])
         nc.vector.tensor_scalar(out=neg_inv_root[:], in0=inv_root[:], scalar1=-1.0, scalar2=None, op0=ALU.mult)
-        along_free = [psum.tile([P, PACK, P], F32, name="spread%d" % half, bufs=1) for half in range(2)]
-        for half in (1, 0):
+
+        def spread_over_partitions(half):
+            along_free = psum.tile([P, PACK, P], F32, tag="spread", bufs=1)
             for k in range(PACK):
                 slot = half * PACK + k
                 nc.tensor.matmul(
-                    out=along_free[half][:, k, :],
+                    out=along_free[:, k, :],
                     lhsT=neg_inv_root[:, slot : slot + 1].to_broadcast([P, P]),
                     rhs=ident[:],
                     start=True,
                     stop=True,
                 )
+            return along_free
 
         def scale_rows(slot, half):
             cols = slice(half * HALF, (half + 1) * HALF)
@@ -175,19 +141,31 @@ def tile_dynamicgraphspatialconv_pa_kernel(tc, x, adj_param, w_cheb0, w_cheb1, o
                 op0=ALU.mult,
             )
 
+        factors = {1: spread_over_partitions(1)}
         for slot in range(SLOTS):
             scale_rows(slot, 1)
-        x_over_nodes(1)
 
-        w_grouped = keep.tile([P, 2, C_OUT, PACK], BF16, align_bytes=64)
-        w_codes = keep.tile([P, 2, C_OUT], U32, align_bytes=64)
-        w_scales = keep.tile([P, 2, C_OUT], U8, align_bytes=64)
-        nc.vector.tensor_copy(out=w_grouped[:], in_=w_raw[:].rearrange("p k j o -> p k o j"))
-        nc.vector.quantize_mx(
-            out=w_codes[:].rearrange("p k o -> p (k o)").bitcast(FP8X4),
-            scales=w_scales[:].rearrange("p k o -> p (k o)"),
-            in_=w_grouped[:].rearrange("p k o j -> p (k o j)"),
-        )
+        xn_codes = keep.tile([P, 2, T, PACK, P], U32, align_bytes=64)
+        xn_scales = keep.tile([P, 2, T, PACK, P], U8, align_bytes=64)
+        for g in (1, 0):
+            for t in range(T):
+                xn_grouped = stage.tile([P, PACK, P, PACK], BF16, align_bytes=64, bufs=3)
+                for jp in range(2):
+                    flipped_x = psum.tile([P, PACK, 2, P], BF16, tag="b", bufs=3)
+                    for v in range(PACK):
+                        nodes_of_slot = x_raw[2 * g + v // 2][:].rearrange("p j (s q t) -> p j s t q", s=2, t=T)
+                        for jj in range(2):
+                            nc.tensor.transpose(
+                                flipped_x[:, v, jj, :], nodes_of_slot[:, 2 * jp + jj, v % 2, t, :], ident_bf[:]
+                            )
+                    nc.scalar.copy(
+                        out=xn_grouped[:, 2 * jp : 2 * jp + 2], in_=flipped_x[:].rearrange("q v jj p -> q jj p v")
+                    )
+                nc.vector.quantize_mx(
+                    out=xn_codes[:, g, t].rearrange("q j p -> q (j p)").bitcast(FP8X4),
+                    scales=xn_scales[:, g, t].rearrange("q j p -> q (j p)"),
+                    in_=xn_grouped[:].rearrange("q j p v -> q (j p v)"),
+                )
 
         xc_codes = keep.tile([P, T, NODES], U32, align_bytes=64)
         xc_scales = keep.tile([P, T, NODES], U8, align_bytes=64)
@@ -202,7 +180,7 @@ def tile_dynamicgraphspatialconv_pa_kernel(tc, x, adj_param, w_cheb0, w_cheb1, o
             nc.vector.tensor_tensor(
                 out=grouped,
                 in0=sym[:, g * PACK : (g + 1) * PACK, h * QUARTER : (h + 1) * QUARTER].rearrange("q v w -> q w v"),
-                in1=along_free[h // 2][:, 2 * (h % 2) : 2 * (h % 2) + 2, :]
+                in1=factors[h // 2][:, 2 * (h % 2) : 2 * (h % 2) + 2, :]
                 .rearrange("q k w -> q (k w)")
                 .unsqueeze(2)
                 .to_broadcast([P, QUARTER, PACK]),
@@ -217,31 +195,59 @@ def tile_dynamicgraphspatialconv_pa_kernel(tc, x, adj_param, w_cheb0, w_cheb1, o
                 in_=grouped.rearrange("q w v -> q (w v)"),
             )
 
-        for h in (2, 3, 0, 1):
+        def columns_of_s(h):
             lower = stage.tile([P, QUARTER, PACK], BF16, align_bytes=64)
             if h >= 2:
                 upper = upper_right[:, (h - 2) * QUARTER : (h - 1) * QUARTER, :]
                 scale_columns(0, h, upper)
                 scale_columns(1, h, lower[:])
             else:
+                for b in range(2):
+                    mirrored = psum.tile([P, PACK, P], BF16, tag="a")
+                    for k in range(PACK):
+                        nc.tensor.transpose(mirrored[:, k, :], upper_right[:, k * P : (k + 1) * P, 2 * h + b], ident_bf[:])
+                    nc.scalar.copy(out=lower[:, b * P : (b + 1) * P, :], in_=mirrored[:].rearrange("w k q -> w q k"))
                 if h == 0:
+                    factors[0] = spread_over_partitions(0)
                     for slot in range(PACK):
                         scale_rows(slot, 0)
                 upper_left = stage.tile([P, QUARTER, PACK], BF16, align_bytes=64)
                 upper = upper_left[:]
                 scale_columns(0, h, upper)
-                for b in range(2):
-                    mirrored = psum.tile([P, PACK, P], BF16, tag="work")
-                    for k in range(PACK):
-                        nc.tensor.transpose(mirrored[:, k, :], upper_right[:, k * P : (k + 1) * P, 2 * h + b], ident_bf[:])
-                    nc.scalar.copy(out=lower[:, b * P : (b + 1) * P, :], in_=mirrored[:].rearrange("w k q -> w q k"))
             quantise_s(0, h, upper)
             quantise_s(1, h, lower[:])
+
+        def x_over_channels(h):
+            xc_grouped = stage.tile([P, T, QUARTER, PACK], BF16, align_bytes=64)
+            for t in range(T):
+                nc.vector.tensor_copy(out=xc_grouped[:, t], in_=x_raw[h][:].rearrange("p j (n t) -> p t n j", t=T)[:, t])
+            for t in range(T):
+                nc.vector.quantize_mx(
+                    out=xc_codes[:, t, h * QUARTER : (h + 1) * QUARTER].bitcast(FP8X4),
+                    scales=xc_scales[:, t, h * QUARTER : (h + 1) * QUARTER],
+                    in_=xc_grouped[:, t].rearrange("p n j -> p (n j)"),
+                )
+
+        columns_of_s(QUARTER_ORDER[0])
+
+        w_grouped = keep.tile([P, 2, C_OUT, PACK], BF16, align_bytes=64)
+        w_codes = keep.tile([P, 2, C_OUT], U32, align_bytes=64)
+        w_scales = keep.tile([P, 2, C_OUT], U8, align_bytes=64)
+        nc.vector.tensor_copy(out=w_grouped[:], in_=w_raw[:].rearrange("p k j o -> p k o j"))
+        nc.vector.quantize_mx(
+            out=w_codes[:].rearrange("p k o -> p (k o)").bitcast(FP8X4),
+            scales=w_scales[:].rearrange("p k o -> p (k o)"),
+            in_=w_grouped[:].rearrange("p k o j -> p (k o j)"),
+        )
+
+        for i, h in enumerate(QUARTER_ORDER):
+            if i + 1 < QUARTERS:
+                columns_of_s(QUARTER_ORDER[i + 1])
             for b in range(2):
                 block = slice((2 * h + b) * P, (2 * h + b + 1) * P)
                 tx_grouped = stage.tile([P, T, P, PACK], BF16, align_bytes=64, bufs=3)
                 for t in range(T):
-                    tx = psum.tile([P, PACK, P], F32, tag="work")
+                    tx = psum.tile([P, PACK, P], F32, tag="a")
                     for j in range(PACK):
                         for g in range(2):
                             nc.tensor.matmul_mx(
@@ -260,17 +266,8 @@ def tile_dynamicgraphspatialconv_pa_kernel(tc, x, adj_param, w_cheb0, w_cheb1, o
                         in_=tx_grouped[:, t].rearrange("p v j -> p (v j)"),
                     )
                 if b == 0:
-                    for t in range(T):
-                        xc_grouped = stage.tile([P, QUARTER, PACK], BF16, align_bytes=64, bufs=3)
-                        nc.vector.tensor_copy(
-                            out=xc_grouped[:], in_=x_raw[h][:].rearrange("p j (n t) -> p t n j", t=T)[:, t]
-                        )
-                        nc.vector.quantize_mx(
-                            out=xc_codes[:, t, h * QUARTER : (h + 1) * QUARTER].bitcast(FP8X4),
-                            scales=xc_scales[:, t, h * QUARTER : (h + 1) * QUARTER],
-                            in_=xc_grouped[:].rearrange("p n j -> p (n j)"),
-                        )
-                both = psum.tile([P, T, C_OUT], F32, tag="both", bufs=2)
+                    x_over_channels(h)
+                both = psum.tile([P, T, C_OUT], F32, tag="b", bufs=3)
                 for t in range(T):
                     nc.tensor.matmul_mx(
                         out=both[:, t, :],

@@ -22,6 +22,8 @@ HALF = NODES // 2
 QUARTERS = 4
 QUARTER = NODES // QUARTERS
 QUARTER_ORDER = (2, 3, 0, 1)
+AHEAD = 2
+LAG = 2
 
 FLOPS = 2 * NODES * NODES * T * C_IN + 2 * 2 * T * NODES * C_IN * C_OUT
 
@@ -95,7 +97,7 @@ def tile_dynamicgraphspatialconv_pa_kernel(tc, x, adj_param, w_cheb0, w_cheb1, o
         for half in range(2):
             for slot in range(PACK):
                 symmetrise(slot, half)
-        mirror_sums = psum.tile([P, PACK, 2], F32, tag="b", bufs=3)
+        mirror_sums = psum.tile([P, PACK, 2], F32, tag="spread", bufs=1)
         for k in range(PACK):
             for slot in range(PACK):
                 nc.tensor.matmul(
@@ -109,14 +111,12 @@ def tile_dynamicgraphspatialconv_pa_kernel(tc, x, adj_param, w_cheb0, w_cheb1, o
             symmetrise(slot, 1)
 
         deg = keep.tile([P, SLOTS], F32)
-        root = keep.tile([P, SLOTS], F32)
+        inv_deg = keep.tile([P, SLOTS], F32)
         inv_root = keep.tile([P, SLOTS], F32)
-        neg_inv_root = keep.tile([P, SLOTS], F32)
         nc.vector.tensor_tensor(out=deg[:, :PACK], in0=deg_parts[:, :PACK, 0], in1=deg_parts[:, :PACK, 1], op=ALU.add)
         nc.vector.tensor_tensor(out=deg[:, PACK:], in0=deg_parts[:, PACK:, 1], in1=mirror_sums[:, :, 0], op=ALU.add)
-        nc.scalar.activation(out=root[:], in_=deg[:], func=ACT.Sqrt)
-        nc.vector.reciprocal(out=inv_root[:], in_=root[:])
-        nc.vector.tensor_scalar(out=neg_inv_root[:], in0=inv_root[:], scalar1=-1.0, scalar2=None, op0=ALU.mult)
+        nc.vector.reciprocal(out=inv_deg[:], in_=deg[:])
+        nc.scalar.activation(out=inv_root[:], in_=inv_deg[:], func=ACT.Sqrt)
 
         def spread_over_partitions(half):
             along_free = psum.tile([P, PACK, P], F32, tag="spread", bufs=1)
@@ -124,7 +124,7 @@ def tile_dynamicgraphspatialconv_pa_kernel(tc, x, adj_param, w_cheb0, w_cheb1, o
                 slot = half * PACK + k
                 nc.tensor.matmul(
                     out=along_free[:, k, :],
-                    lhsT=neg_inv_root[:, slot : slot + 1].to_broadcast([P, P]),
+                    lhsT=inv_root[:, slot : slot + 1].to_broadcast([P, P]),
                     rhs=ident[:],
                     start=True,
                     stop=True,
@@ -137,8 +137,9 @@ def tile_dynamicgraphspatialconv_pa_kernel(tc, x, adj_param, w_cheb0, w_cheb1, o
                 out=sym[:, slot, cols],
                 in0=sym[:, slot, cols],
                 scalar1=inv_root[:, slot : slot + 1],
-                scalar2=None,
+                scalar2=-1.0,
                 op0=ALU.mult,
+                op1=ALU.mult,
             )
 
         factors = {1: spread_over_partitions(1)}
@@ -151,7 +152,10 @@ def tile_dynamicgraphspatialconv_pa_kernel(tc, x, adj_param, w_cheb0, w_cheb1, o
             for t in range(T):
                 xn_grouped = stage.tile([P, PACK, P, PACK], BF16, align_bytes=64, bufs=3)
                 for jp in range(2):
-                    flipped_x = psum.tile([P, PACK, 2, P], BF16, tag="b", bufs=3)
+                    if g == 1:
+                        flipped_x = psum.tile([P, PACK, 2, P], BF16, tag="b", bufs=3)
+                    else:
+                        flipped_x = psum.tile([P, PACK, 2, P], BF16, tag="a")
                     for v in range(PACK):
                         nodes_of_slot = x_raw[2 * g + v // 2][:].rearrange("p j (s q t) -> p j s t q", s=2, t=T)
                         for jj in range(2):
@@ -228,7 +232,8 @@ def tile_dynamicgraphspatialconv_pa_kernel(tc, x, adj_param, w_cheb0, w_cheb1, o
                     in_=xc_grouped[:, t].rearrange("p n j -> p (n j)"),
                 )
 
-        columns_of_s(QUARTER_ORDER[0])
+        for i in range(AHEAD):
+            columns_of_s(QUARTER_ORDER[i])
 
         w_grouped = keep.tile([P, 2, C_OUT, PACK], BF16, align_bytes=64)
         w_codes = keep.tile([P, 2, C_OUT], U32, align_bytes=64)
@@ -240,53 +245,61 @@ def tile_dynamicgraphspatialconv_pa_kernel(tc, x, adj_param, w_cheb0, w_cheb1, o
             in_=w_grouped[:].rearrange("p k o j -> p (k o j)"),
         )
 
-        for i, h in enumerate(QUARTER_ORDER):
-            if i + 1 < QUARTERS:
-                columns_of_s(QUARTER_ORDER[i + 1])
-            for b in range(2):
-                block = slice((2 * h + b) * P, (2 * h + b + 1) * P)
-                tx_grouped = stage.tile([P, T, P, PACK], BF16, align_bytes=64, bufs=3)
-                for t in range(T):
-                    tx = psum.tile([P, PACK, P], F32, tag="a")
-                    for j in range(PACK):
-                        for g in range(2):
-                            nc.tensor.matmul_mx(
-                                out=tx[:, j, :],
-                                lhsT=xn_codes[:, g, t, j, :].bitcast(FP8X4),
-                                lhsT_scale=xn_scales[:, g, t, j, :],
-                                rhs=s_codes[:, g, block].bitcast(FP8X4),
-                                rhs_scale=s_scales[:, g, block],
-                                start=(g == 0),
-                                stop=(g == 1),
-                            )
-                    nc.scalar.copy(out=tx_grouped[:, t], in_=tx[:].rearrange("p j v -> p v j"))
-                    nc.vector.quantize_mx(
-                        out=tx_codes[:, t, block].bitcast(FP8X4),
-                        scales=tx_scales[:, t, block],
-                        in_=tx_grouped[:, t].rearrange("p v j -> p (v j)"),
-                    )
-                if b == 0:
-                    x_over_channels(h)
-                both = psum.tile([P, T, C_OUT], F32, tag="b", bufs=3)
-                for t in range(T):
-                    nc.tensor.matmul_mx(
-                        out=both[:, t, :],
-                        lhsT=xc_codes[:, t, block].bitcast(FP8X4),
-                        lhsT_scale=xc_scales[:, t, block],
-                        rhs=w_codes[:, 0, :].bitcast(FP8X4),
-                        rhs_scale=w_scales[:, 0, :],
-                        start=True,
-                        stop=False,
-                    )
-                    nc.tensor.matmul_mx(
-                        out=both[:, t, :],
-                        lhsT=tx_codes[:, t, block].bitcast(FP8X4),
-                        lhsT_scale=tx_scales[:, t, block],
-                        rhs=w_codes[:, 1, :].bitcast(FP8X4),
-                        rhs_scale=w_scales[:, 1, :],
-                        start=False,
-                        stop=True,
-                    )
-                result = stage.tile([P, T, C_OUT], F32, bufs=3)
-                nc.scalar.copy(out=result[:], in_=both[:])
-                nc.sync.dma_start(out=out_rows[2 * h + b], in_=result[:])
+        def tx1_of_block(block):
+            tx_grouped = stage.tile([P, T, P, PACK], BF16, align_bytes=64, bufs=3)
+            for t in range(T):
+                tx = psum.tile([P, PACK, P], F32, tag="a")
+                for j in range(PACK):
+                    for g in range(2):
+                        nc.tensor.matmul_mx(
+                            out=tx[:, j, :],
+                            lhsT=xn_codes[:, g, t, j, :].bitcast(FP8X4),
+                            lhsT_scale=xn_scales[:, g, t, j, :],
+                            rhs=s_codes[:, g, block].bitcast(FP8X4),
+                            rhs_scale=s_scales[:, g, block],
+                            start=(g == 0),
+                            stop=(g == 1),
+                        )
+                nc.scalar.copy(out=tx_grouped[:, t], in_=tx[:].rearrange("p j v -> p v j"))
+                nc.vector.quantize_mx(
+                    out=tx_codes[:, t, block].bitcast(FP8X4),
+                    scales=tx_scales[:, t, block],
+                    in_=tx_grouped[:, t].rearrange("p v j -> p (v j)"),
+                )
+
+        def result_of_block(number, block):
+            both = psum.tile([P, T, C_OUT], F32, tag="b", bufs=3)
+            for t in range(T):
+                nc.tensor.matmul_mx(
+                    out=both[:, t, :],
+                    lhsT=xc_codes[:, t, block].bitcast(FP8X4),
+                    lhsT_scale=xc_scales[:, t, block],
+                    rhs=w_codes[:, 0, :].bitcast(FP8X4),
+                    rhs_scale=w_scales[:, 0, :],
+                    start=True,
+                    stop=False,
+                )
+                nc.tensor.matmul_mx(
+                    out=both[:, t, :],
+                    lhsT=tx_codes[:, t, block].bitcast(FP8X4),
+                    lhsT_scale=tx_scales[:, t, block],
+                    rhs=w_codes[:, 1, :].bitcast(FP8X4),
+                    rhs_scale=w_scales[:, 1, :],
+                    start=False,
+                    stop=True,
+                )
+            result = stage.tile([P, T, C_OUT], F32, bufs=3)
+            nc.scalar.copy(out=result[:], in_=both[:])
+            nc.sync.dma_start(out=out_rows[number], in_=result[:])
+
+        numbers = [2 * h + b for h in QUARTER_ORDER for b in range(2)]
+        blocks = [slice(number * P, (number + 1) * P) for number in numbers]
+        for i in range(len(numbers) + LAG):
+            if i < len(numbers):
+                if i % 2 == 0 and i // 2 + AHEAD < QUARTERS:
+                    columns_of_s(QUARTER_ORDER[i // 2 + AHEAD])
+                tx1_of_block(blocks[i])
+                if i % 2 == 0:
+                    x_over_channels(numbers[i] // 2)
+            if i >= LAG:
+                result_of_block(numbers[i - LAG], blocks[i - LAG])

@@ -152,10 +152,7 @@ def tile_dynamicgraphspatialconv_pa_kernel(tc, x, adj_param, w_cheb0, w_cheb1, o
             for t in range(T):
                 xn_grouped = stage.tile([P, PACK, P, PACK], BF16, align_bytes=64, bufs=3)
                 for jp in range(2):
-                    if g == 1:
-                        flipped_x = psum.tile([P, PACK, 2, P], BF16, tag="b", bufs=3)
-                    else:
-                        flipped_x = psum.tile([P, PACK, 2, P], BF16, tag="a")
+                    flipped_x = psum.tile([P, PACK, 2, P], BF16, tag="b", bufs=3)
                     for v in range(PACK):
                         nodes_of_slot = x_raw[2 * g + v // 2][:].rearrange("p j (s q t) -> p j s t q", s=2, t=T)
                         for jj in range(2):

@@ -39,8 +39,6 @@ def tile_dynamicgraphspatialconv_pa_kernel(tc, x, adj_param, w_cheb0, w_cheb1, o
         make_identity(nc, ident[:])
         ident_bf = keep.tile([P, P], BF16)
         make_identity(nc, ident_bf[:])
-        ones = keep.tile([P, 2], F32)
-        nc.vector.memset(ones[:], 1.0)
 
         adj_rows = adj_param.rearrange("(h s q) m -> h q s m", h=QUARTERS, q=P)
         x_rows = x[0].rearrange("(p j) (h n) t -> h p j (n t)", j=PACK, h=QUARTERS)
@@ -60,7 +58,12 @@ def tile_dynamicgraphspatialconv_pa_kernel(tc, x, adj_param, w_cheb0, w_cheb1, o
 
         def sigmoid(slot, half):
             cols = slice(half * HALF, (half + 1) * HALF)
-            nc.scalar.activation(out=sig[:, slot, cols], in_=adj_sb[slot // 2][:, slot % 2, cols], func=ACT.Sigmoid)
+            nc.scalar.activation(
+                out=sig[:, slot, cols],
+                in_=adj_sb[slot // 2][:, slot % 2, cols],
+                func=ACT.Sigmoid,
+                accum_out=(deg_parts[:, slot, 0:1] if (slot >= PACK and half == 0) else None),
+            )
             if slot // PACK == half:
                 diagonal_block = sig[:, slot, slot * P : (slot + 1) * P]
                 nc.gpsimd.affine_select(
@@ -91,30 +94,34 @@ def tile_dynamicgraphspatialconv_pa_kernel(tc, x, adj_param, w_cheb0, w_cheb1, o
         for half in range(2):
             for slot in range(SLOTS):
                 sigmoid(slot, half)
+        turned_sums = keep.tile([P, PACK], F32)
+        for k in range(PACK):
+            turned = psum.tile([P, PACK, P], BF16, tag="a")
+            for slot in range(PACK):
+                nc.tensor.transpose(
+                    turned[:, slot, :], adj_sb[slot // 2][:, slot % 2, (PACK + k) * P : (PACK + k + 1) * P], ident_bf[:]
+                )
+            unused = stage.tile([P, HALF], F32)
+            nc.scalar.activation(
+                out=unused[:],
+                in_=turned[:].rearrange("q s w -> q (s w)"),
+                func=ACT.Sigmoid,
+                accum_out=turned_sums[:, k : k + 1],
+            )
         warm = keep.tile([P, 1], F32)
         nc.scalar.activation(out=warm[:], in_=sig[:, SLOTS - 1, NODES - 1 : NODES], func=ACT.Sqrt)
 
         for half in range(2):
             for slot in range(PACK):
                 symmetrise(slot, half)
-        mirror_sums = psum.tile([P, PACK, 2], F32, tag="spread", bufs=1)
-        for k in range(PACK):
-            for slot in range(PACK):
-                nc.tensor.matmul(
-                    out=mirror_sums[:, k, :],
-                    lhsT=sym[:, slot, (PACK + k) * P : (PACK + k + 1) * P],
-                    rhs=ones[:],
-                    start=(slot == 0),
-                    stop=(slot == PACK - 1),
-                )
         for slot in range(PACK, SLOTS):
             symmetrise(slot, 1)
 
         deg = keep.tile([P, SLOTS], F32)
         inv_deg = keep.tile([P, SLOTS], F32)
         inv_root = keep.tile([P, SLOTS], F32)
-        nc.vector.tensor_tensor(out=deg[:, :PACK], in0=deg_parts[:, :PACK, 0], in1=deg_parts[:, :PACK, 1], op=ALU.add)
-        nc.vector.tensor_tensor(out=deg[:, PACK:], in0=deg_parts[:, PACK:, 1], in1=mirror_sums[:, :, 0], op=ALU.add)
+        nc.vector.tensor_tensor(out=deg[:], in0=deg_parts[:, :, 0], in1=deg_parts[:, :, 1], op=ALU.add)
+        nc.vector.tensor_tensor(out=deg[:, PACK:], in0=deg[:, PACK:], in1=turned_sums[:], op=ALU.add)
         nc.vector.reciprocal(out=inv_deg[:], in_=deg[:])
         nc.scalar.activation(out=inv_root[:], in_=inv_deg[:], func=ACT.Sqrt)
 
@@ -122,13 +129,7 @@ def tile_dynamicgraphspatialconv_pa_kernel(tc, x, adj_param, w_cheb0, w_cheb1, o
             along_free = psum.tile([P, PACK, P], F32, tag="spread", bufs=1)
             for k in range(PACK):
                 slot = half * PACK + k
-                nc.tensor.matmul(
-                    out=along_free[:, k, :],
-                    lhsT=inv_root[:, slot : slot + 1].to_broadcast([P, P]),
-                    rhs=ident[:],
-                    start=True,
-                    stop=True,
-                )
+                nc.tensor.transpose(along_free[:, k, :], inv_root[:, slot : slot + 1].to_broadcast([P, P]), ident[:])
             return along_free
 
         def scale_rows(slot, half):

@@ -44,13 +44,13 @@ def tile_dynamicgraphspatialconv_pa_kernel(tc, x, adj_param, w_cheb0, w_cheb1, o
         x_rows = x[0].rearrange("(p j) (h n) t -> h p j (n t)", j=PACK, h=QUARTERS)
         adj_sb = [keep.tile([P, 2, NODES], BF16, name="adj%d" % h) for h in range(QUARTERS)]
         x_raw = [keep.tile([P, PACK, QUARTER * T], BF16, name="xraw%d" % h) for h in range(QUARTERS)]
-        for h in range(QUARTERS):
-            nc.sync.dma_start(out=adj_sb[h][:], in_=adj_rows[h])
+        for slot in range(SLOTS):
+            nc.sync.dma_start(out=adj_sb[slot // 2][:, slot % 2, :], in_=adj_rows[slot // 2][:, slot % 2, :])
+        w_raw = keep.tile([P, 2, PACK, C_OUT], BF16)
+        nc.sync.dma_start(out=w_raw[:, 0], in_=w_cheb0.rearrange("(p j) o -> p j o", j=PACK))
+        nc.sync.dma_start(out=w_raw[:, 1], in_=w_cheb1.rearrange("(p j) o -> p j o", j=PACK))
         for h in QUARTER_ORDER:
             nc.sync.dma_start(out=x_raw[h][:], in_=x_rows[h])
-        w_raw = keep.tile([P, 2, PACK, C_OUT], BF16)
-        nc.scalar.dma_start(out=w_raw[:, 0], in_=w_cheb0.rearrange("(p j) o -> p j o", j=PACK))
-        nc.scalar.dma_start(out=w_raw[:, 1], in_=w_cheb1.rearrange("(p j) o -> p j o", j=PACK))
 
         sig = keep.tile([P, SLOTS, NODES], F32)
         sym = keep.tile([P, SLOTS, NODES], F32)

@@ -96,7 +96,7 @@ def tile_dynamicgraphspatialconv_pa_kernel(tc, x, adj_param, w_cheb0, w_cheb1, o
                 sigmoid(slot, half)
         turned_sums = keep.tile([P, PACK], F32)
         for k in range(PACK):
-            turned = psum.tile([P, PACK, P], BF16, tag="a")
+            turned = psum.tile([P, PACK, P], BF16, tag="b", bufs=3)
             for slot in range(PACK):
                 nc.tensor.transpose(
                     turned[:, slot, :], adj_sb[slot // 2][:, slot % 2, (PACK + k) * P : (PACK + k + 1) * P], ident_bf[:]

@@ -44,7 +44,10 @@ def tile_dynamicgraphspatialconv_pa_kernel(tc, x, adj_param, w_cheb0, w_cheb1, o
         x_rows = x[0].rearrange("(p j) (h n) t -> h p j (n t)", j=PACK, h=QUARTERS)
         adj_sb = [keep.tile([P, 2, NODES], BF16, name="adj%d" % h) for h in range(QUARTERS)]
         x_raw = [keep.tile([P, PACK, QUARTER * T], BF16, name="xraw%d" % h) for h in range(QUARTERS)]
-        for slot in range(SLOTS):
+        for half in range(2):
+            cols = slice(half * HALF, (half + 1) * HALF)
+            nc.sync.dma_start(out=adj_sb[0][:, 0, cols], in_=adj_rows[0][:, 0, cols])
+        for slot in range(1, SLOTS):
             nc.sync.dma_start(out=adj_sb[slot // 2][:, slot % 2, :], in_=adj_rows[slot // 2][:, slot % 2, :])
         w_raw = keep.tile([P, 2, PACK, C_OUT], BF16)
         nc.sync.dma_start(out=w_raw[:, 0], in_=w_cheb0.rearrange("(p j) o -> p j o", j=PACK))

@@ -10,6 +10,7 @@ U8 = mybir.dt.uint8
 FP8X4 = mybir.dt.float8_e4m3fn_x4
 ACT = mybir.ActivationFunctionType
 ALU = mybir.AluOpType
+AX = mybir.AxisListType
 
 P = 128
 PACK = 4
@@ -21,9 +22,8 @@ SLOTS = NODES // P
 HALF = NODES // 2
 QUARTERS = 4
 QUARTER = NODES // QUARTERS
-QUARTER_ORDER = (2, 3, 0, 1)
-AHEAD = 2
-LAG = 2
+L, R = 0, 1
+UPPER, LOWER = range(PACK), range(PACK, SLOTS)
 
 FLOPS = 2 * NODES * NODES * T * C_IN + 2 * 2 * T * NODES * C_IN * C_OUT
 
@@ -33,274 +33,399 @@ def tile_dynamicgraphspatialconv_pa_kernel(tc, x, adj_param, w_cheb0, w_cheb1, o
     with ExitStack() as stack:
         keep = stack.enter_context(tc.tile_pool(name="keep", bufs=1))
         stage = stack.enter_context(tc.tile_pool(name="stage", bufs=2))
-        psum = stack.enter_context(tc.psum_pool(name="psum", bufs=4))
+        psum = stack.enter_context(tc.psum_pool(name="psum", bufs=1))
+        stack.enter_context(tc.manual_schedule())
+
+        adj_rows = adj_param.rearrange("(s q) m -> s q m", q=P)
+        adj_sb = [keep.tile([P, 2, NODES], BF16, name="adj%d" % i, tag="adj%d" % i, align_bytes=64) for i in range(PACK)]
+
+        def adj_of(slot):
+            return adj_sb[slot // 2][:, slot % 2]
+
+        for half in range(2):
+            cols = slice(half * HALF, (half + 1) * HALF)
+            nc.sync.dma_start(out=adj_of(0)[:, cols], in_=adj_rows[0][:, cols])
+        x_rows = x[0].rearrange("(p j) (h n) t -> h p j (n t)", j=PACK, h=QUARTERS)
+        x_raw = [keep.tile([P, PACK, QUARTER * T], BF16, name="xraw%d" % h) for h in range(QUARTERS)]
+        for slot in range(1, SLOTS):
+            nc.sync.dma_start(out=adj_of(slot), in_=adj_rows[slot])
+            if slot < 3:
+                cols = slice((slot - 1) * P * T, slot * P * T)
+                nc.sync.dma_start(out=x_raw[2][:, :, cols], in_=x_rows[2][:, :, cols])
+        x_turn_rows = x[0].rearrange("(j G e) (s n) t -> j (e s) G (n t)", j=PACK, e=16, s=SLOTS)
+        x_turn = [keep.tile([P, SLOTS, P * T], BF16, name="xturn%d" % j) for j in range(PACK)]
+        for j in range(PACK):
+            nc.sync.dma_start(out=x_turn[j][:], in_=x_turn_rows[j])
+        w_raw = keep.tile([P, 2, PACK, C_OUT], BF16)
+        nc.sync.dma_start(out=w_raw[:, 0], in_=w_cheb0.rearrange("(p j) o -> p j o", j=PACK))
+        nc.sync.dma_start(out=w_raw[:, 1], in_=w_cheb1.rearrange("(j p) o -> p j o", j=PACK))
+        for h in (3, 0, 1):
+            nc.sync.dma_start(out=x_raw[h][:], in_=x_rows[h])
 
         ident = keep.tile([P, P], F32)
         make_identity(nc, ident[:])
         ident_bf = keep.tile([P, P], BF16)
         make_identity(nc, ident_bf[:])
+        deg_parts = keep.tile([P, SLOTS, 3], F32)
+        nc.vector.memset(deg_parts[:], 0.0)
 
-        adj_rows = adj_param.rearrange("(h s q) m -> h q s m", h=QUARTERS, q=P)
-        x_rows = x[0].rearrange("(p j) (h n) t -> h p j (n t)", j=PACK, h=QUARTERS)
-        adj_sb = [keep.tile([P, 2, NODES], BF16, name="adj%d" % h) for h in range(QUARTERS)]
-        x_raw = [keep.tile([P, PACK, QUARTER * T], BF16, name="xraw%d" % h) for h in range(QUARTERS)]
-        for half in range(2):
-            cols = slice(half * HALF, (half + 1) * HALF)
-            nc.sync.dma_start(out=adj_sb[0][:, 0, cols], in_=adj_rows[0][:, 0, cols])
-        for slot in range(1, SLOTS):
-            nc.sync.dma_start(out=adj_sb[slot // 2][:, slot % 2, :], in_=adj_rows[slot // 2][:, slot % 2, :])
-        w_raw = keep.tile([P, 2, PACK, C_OUT], BF16)
-        nc.sync.dma_start(out=w_raw[:, 0], in_=w_cheb0.rearrange("(p j) o -> p j o", j=PACK))
-        nc.sync.dma_start(out=w_raw[:, 1], in_=w_cheb1.rearrange("(p j) o -> p j o", j=PACK))
-        for h in QUARTER_ORDER:
-            nc.sync.dma_start(out=x_raw[h][:], in_=x_rows[h])
-
-        sig = keep.tile([P, SLOTS, NODES], F32)
-        sym = keep.tile([P, SLOTS, NODES], F32)
-        deg_parts = keep.tile([P, SLOTS, 2], F32)
-
-        def sigmoid(slot, half):
-            cols = slice(half * HALF, (half + 1) * HALF)
-            nc.scalar.activation(
-                out=sig[:, slot, cols],
-                in_=adj_sb[slot // 2][:, slot % 2, cols],
-                func=ACT.Sigmoid,
-                accum_out=(deg_parts[:, slot, 0:1] if (slot >= PACK and half == 0) else None),
-            )
-            if slot // PACK == half:
-                diagonal_block = sig[:, slot, slot * P : (slot + 1) * P]
-                nc.gpsimd.affine_select(
-                    out=diagonal_block,
-                    in_=diagonal_block,
-                    pattern=[[-1, P]],
-                    compare_op=ALU.not_equal,
-                    fill=0.0,
-                    base=0,
-                    channel_multiplier=1,
-                )
-
-        def symmetrise(slot, half):
-            cols = slice(half * HALF, (half + 1) * HALF)
-            flipped = psum.tile([P, PACK, P], F32, tag="a")
-            for k in range(PACK):
-                nc.tensor.transpose(flipped[:, k, :], sig[:, half * PACK + k, slot * P : (slot + 1) * P], ident[:])
-            nc.vector.scalar_tensor_tensor(
-                out=sym[:, slot, cols],
-                in0=flipped[:].rearrange("q k w -> q (k w)"),
-                scalar=1.0,
-                in1=sig[:, slot, cols],
-                op0=ALU.mult,
-                op1=ALU.add,
-                accum_out=deg_parts[:, slot, half : half + 1],
-            )
-
-        for half in range(2):
-            for slot in range(SLOTS):
-                sigmoid(slot, half)
-        turned_sums = keep.tile([P, PACK], F32)
-        for k in range(PACK):
-            turned = psum.tile([P, PACK, P], BF16, tag="b", bufs=3)
-            for slot in range(PACK):
-                nc.tensor.transpose(
-                    turned[:, slot, :], adj_sb[slot // 2][:, slot % 2, (PACK + k) * P : (PACK + k + 1) * P], ident_bf[:]
-                )
-            unused = stage.tile([P, HALF], F32)
-            nc.scalar.activation(
-                out=unused[:],
-                in_=turned[:].rearrange("q s w -> q (s w)"),
-                func=ACT.Sigmoid,
-                accum_out=turned_sums[:, k : k + 1],
-            )
-        warm = keep.tile([P, 1], F32)
-        nc.scalar.activation(out=warm[:], in_=sig[:, SLOTS - 1, NODES - 1 : NODES], func=ACT.Sqrt)
-
-        for half in range(2):
-            for slot in range(PACK):
-                symmetrise(slot, half)
-        for slot in range(PACK, SLOTS):
-            symmetrise(slot, 1)
-
+        sig = keep.tile([P, SLOTS, NODES], F32, name="sig", tag="sig", align_bytes=64)
+        sym_right = keep.tile([P, SLOTS, HALF], F32)
+        sym_left = keep.tile([P, PACK, HALF], F32)
+        col_sums = keep.tile([P, 3, HALF], F32)
+        xn_codes = keep.tile([P, T, PACK, 2, P], U32, align_bytes=64)
+        xn_scales = keep.tile([P, T, PACK, 2, P], U8, align_bytes=64)
+        xc_codes = keep.tile([P, T, NODES], U32, align_bytes=64)
+        xc_scales = keep.tile([P, T, NODES], U8, align_bytes=64)
+        s_codes = keep.tile([P, QUARTERS, 2, QUARTER], U32, align_bytes=64)
+        s_scales = keep.tile([P, QUARTERS, 2, QUARTER], U8, align_bytes=64)
+        tx_codes = keep.tile([P, T, NODES], U32, align_bytes=64)
+        tx_scales = keep.tile([P, T, NODES], U8, align_bytes=64)
+        s_grouped = {h: keep.tile([P, 2, QUARTER, PACK], BF16, name="s%d" % h, align_bytes=64) for h in (2, 3)}
+        inv_root = keep.tile([P, SLOTS], F32)
         deg = keep.tile([P, SLOTS], F32)
         inv_deg = keep.tile([P, SLOTS], F32)
-        inv_root = keep.tile([P, SLOTS], F32)
-        nc.vector.tensor_tensor(out=deg[:], in0=deg_parts[:, :, 0], in1=deg_parts[:, :, 1], op=ALU.add)
-        nc.vector.tensor_tensor(out=deg[:, PACK:], in0=deg[:, PACK:], in1=turned_sums[:], op=ALU.add)
-        nc.vector.reciprocal(out=inv_deg[:], in_=deg[:])
-        nc.scalar.activation(out=inv_root[:], in_=inv_deg[:], func=ACT.Sqrt)
+        w_grouped = keep.tile([P, 2, C_OUT, PACK], BF16, align_bytes=64)
+        w_codes = keep.tile([P, 2, C_OUT], U32, align_bytes=64)
+        w_scales = keep.tile([P, 2, C_OUT], U8, align_bytes=64)
+        out_rows = out[0].rearrange("t (b q) o -> b q t o", q=P)
 
-        def spread_over_partitions(half):
-            along_free = psum.tile([P, PACK, P], F32, tag="spread", bufs=1)
+        xc_early = keep.tile([P, T, QUARTER, PACK], BF16, align_bytes=64)
+        xc_grouped = {2: xc_early}
+
+        def bank(number, shape=(P, PACK, P), dtype=F32):
+            return psum.tile(list(shape), dtype, name="bank%d" % number, tag="bank%d" % number)
+
+        def columns(half):
+            return slice(half * HALF, (half + 1) * HALF)
+
+        def quarter(h):
+            return slice(h * QUARTER, (h + 1) * QUARTER)
+
+        def block_of(b):
+            return slice(b * P, (b + 1) * P)
+
+        def sigmoid(slot, half):
+            nc.scalar.activation(
+                out=sig[:, slot, columns(half)],
+                in_=adj_of(slot)[:, columns(half)],
+                func=ACT.Sigmoid,
+                accum_out=(deg_parts[:, slot, 0:1] if (slot in LOWER and half == L) else None),
+            )
+
+        def fill_diagonal(block, fill):
+            nc.gpsimd.affine_select(
+                out=block,
+                in_=block,
+                pattern=[[-1, P]],
+                compare_op=ALU.not_equal,
+                fill=fill,
+                base=0,
+                channel_multiplier=1,
+            )
+
+        def turn_row(slot, column_slots, banks):
+            for turned, column_slot in zip(banks, column_slots):
+                nc.tensor.transpose(turned[:, slot % PACK, :], sig[:, slot, block_of(column_slot)], ident[:])
+
+        def add(turned, slot, half):
+            rows = sym_left if half == L else sym_right
+            column = 0 if half == L else 1
+            nc.vector.scalar_tensor_tensor(
+                out=rows[:, slot],
+                in0=turned[:].rearrange("q k w -> q (k w)"),
+                scalar=1.0,
+                in1=sig[:, slot, columns(half)],
+                op0=ALU.mult,
+                op1=ALU.add,
+                accum_out=deg_parts[:, slot, column : column + 1],
+            )
+
+        def add_column_sums(turned):
+            unused = stage.tile([P, PACK, P], F32, name="unused", bufs=1)
+            for k in range(PACK):
+                nc.tensor.transpose(turned[:, k, :], col_sums[:, 2, block_of(k)], ident[:])
+            for k in range(PACK):
+                nc.scalar.activation(
+                    out=unused[:, k],
+                    in_=turned[:, k, :],
+                    func=ACT.Copy,
+                    accum_out=deg_parts[:, PACK + k, 2:3],
+                )
+
+        def spread(half, along_free):
             for k in range(PACK):
                 slot = half * PACK + k
                 nc.tensor.transpose(along_free[:, k, :], inv_root[:, slot : slot + 1].to_broadcast([P, P]), ident[:])
-            return along_free
 
-        def scale_rows(slot, half):
-            cols = slice(half * HALF, (half + 1) * HALF)
-            nc.vector.tensor_scalar(
-                out=sym[:, slot, cols],
-                in0=sym[:, slot, cols],
+        def scale_rows(engine, rows, slot, cols):
+            engine.tensor_scalar(
+                out=rows[:, slot, cols],
+                in0=rows[:, slot, cols],
                 scalar1=inv_root[:, slot : slot + 1],
                 scalar2=-1.0,
                 op0=ALU.mult,
                 op1=ALU.mult,
             )
 
-        factors = {1: spread_over_partitions(1)}
-        for slot in range(SLOTS):
-            scale_rows(slot, 1)
-
-        xn_codes = keep.tile([P, 2, T, PACK, P], U32, align_bytes=64)
-        xn_scales = keep.tile([P, 2, T, PACK, P], U8, align_bytes=64)
-        for g in (1, 0):
-            for t in range(T):
-                xn_grouped = stage.tile([P, PACK, P, PACK], BF16, align_bytes=64, bufs=3)
-                for jp in range(2):
-                    flipped_x = psum.tile([P, PACK, 2, P], BF16, tag="b", bufs=3)
-                    for v in range(PACK):
-                        nodes_of_slot = x_raw[2 * g + v // 2][:].rearrange("p j (s q t) -> p j s t q", s=2, t=T)
-                        for jj in range(2):
-                            nc.tensor.transpose(
-                                flipped_x[:, v, jj, :], nodes_of_slot[:, 2 * jp + jj, v % 2, t, :], ident_bf[:]
-                            )
-                    nc.scalar.copy(
-                        out=xn_grouped[:, 2 * jp : 2 * jp + 2], in_=flipped_x[:].rearrange("q v jj p -> q jj p v")
-                    )
-                nc.vector.quantize_mx(
-                    out=xn_codes[:, g, t].rearrange("q j p -> q (j p)").bitcast(FP8X4),
-                    scales=xn_scales[:, g, t].rearrange("q j p -> q (j p)"),
-                    in_=xn_grouped[:].rearrange("q j p v -> q (j p v)"),
-                )
-
-        xc_codes = keep.tile([P, T, NODES], U32, align_bytes=64)
-        xc_scales = keep.tile([P, T, NODES], U8, align_bytes=64)
-        s_codes = keep.tile([P, 2, NODES], U32, align_bytes=64)
-        s_scales = keep.tile([P, 2, NODES], U8, align_bytes=64)
-        tx_codes = keep.tile([P, T, NODES], U32, align_bytes=64)
-        tx_scales = keep.tile([P, T, NODES], U8, align_bytes=64)
-        upper_right = keep.tile([P, HALF, PACK], BF16, align_bytes=64)
-        out_rows = out[0].rearrange("t (b q) o -> b q t o", q=P)
-
-        def scale_columns(g, h, grouped):
+        def scale_columns(g, h):
+            rows = sym_left if h < 2 else sym_right
+            part = h % 2
             nc.vector.tensor_tensor(
-                out=grouped,
-                in0=sym[:, g * PACK : (g + 1) * PACK, h * QUARTER : (h + 1) * QUARTER].rearrange("q v w -> q w v"),
-                in1=factors[h // 2][:, 2 * (h % 2) : 2 * (h % 2) + 2, :]
+                out=s_grouped[h][:, g],
+                in0=rows[:, g * PACK : (g + 1) * PACK, quarter(part)].rearrange("q v w -> q w v"),
+                in1=factors[h // 2][:, 2 * part : 2 * part + 2, :]
                 .rearrange("q k w -> q (k w)")
                 .unsqueeze(2)
                 .to_broadcast([P, QUARTER, PACK]),
                 op=ALU.mult,
             )
 
-        def quantise_s(g, h, grouped):
-            cols = slice(h * QUARTER, (h + 1) * QUARTER)
+        def quantise_s(h):
             nc.vector.quantize_mx(
-                out=s_codes[:, g, cols].bitcast(FP8X4),
-                scales=s_scales[:, g, cols],
-                in_=grouped.rearrange("q w v -> q (w v)"),
+                out=s_codes[:, h].rearrange("q g w -> q (g w)").bitcast(FP8X4),
+                scales=s_scales[:, h].rearrange("q g w -> q (g w)"),
+                in_=s_grouped[h][:].rearrange("q g w v -> q (g w v)"),
             )
 
-        def columns_of_s(h):
-            lower = stage.tile([P, QUARTER, PACK], BF16, align_bytes=64)
-            if h >= 2:
-                upper = upper_right[:, (h - 2) * QUARTER : (h - 1) * QUARTER, :]
-                scale_columns(0, h, upper)
-                scale_columns(1, h, lower[:])
-            else:
-                for b in range(2):
-                    mirrored = psum.tile([P, PACK, P], BF16, tag="a")
-                    for k in range(PACK):
-                        nc.tensor.transpose(mirrored[:, k, :], upper_right[:, k * P : (k + 1) * P, 2 * h + b], ident_bf[:])
-                    nc.scalar.copy(out=lower[:, b * P : (b + 1) * P, :], in_=mirrored[:].rearrange("w k q -> w q k"))
-                if h == 0:
-                    factors[0] = spread_over_partitions(0)
-                    for slot in range(PACK):
-                        scale_rows(slot, 0)
-                upper_left = stage.tile([P, QUARTER, PACK], BF16, align_bytes=64)
-                upper = upper_left[:]
-                scale_columns(0, h, upper)
-            quantise_s(0, h, upper)
-            quantise_s(1, h, lower[:])
+        def mirror(b, mirrored):
+            for k in range(PACK):
+                upper = s_grouped[2 + k // 2][:, 0, (k % 2) * P : (k % 2 + 1) * P, b]
+                nc.tensor.transpose(mirrored[:, k, :], upper, ident_bf[:])
+            nc.scalar.copy(
+                out=s_grouped[b // 2][:, 1, (b % 2) * P : (b % 2 + 1) * P, :],
+                in_=mirrored[:].rearrange("w k q -> w q k"),
+            )
 
-        def x_over_channels(h):
-            xc_grouped = stage.tile([P, T, QUARTER, PACK], BF16, align_bytes=64)
+        xn_grouped = {}
+
+        def turn_x(j, t, turned):
+            for G in range(SLOTS):
+                block = x_turn[j][:, G, :].rearrange("p (n t) -> p t n", t=T)[:, t, :]
+                if G % 2 == 0:
+                    nc.tensor.matmul(turned[:, G, :], lhsT=block, rhs=ident_bf[:], start=True, stop=True)
+                else:
+                    nc.tensor.transpose(turned[:, G, :], block, ident_bf[:])
+
+        def group_x(j, t, turned):
+            if j % 2 == 0:
+                i = 3 * (j // 2) + t
+                tag = "adj%d" % i if i < PACK else "xn%d" % i
+                xn_grouped[j // 2, t] = keep.tile([P, 2, 2, P, PACK], BF16, name="xn%d" % i, tag=tag, align_bytes=64)
+            nc.scalar.copy(
+                out=xn_grouped[j // 2, t][:, j % 2].rearrange("q g c v -> q g (c v)").bitcast(F32),
+                in_=turned[:].rearrange("q G c -> q (G c)").bitcast(F32).rearrange("q (c g w) -> q g c w", g=2, w=2),
+            )
+
+        def quantise_x(pair, t):
+            js = slice(2 * pair, 2 * pair + 2)
+            nc.vector.quantize_mx(
+                out=xn_codes[:, t, js].rearrange("q j g p -> q (j g p)").bitcast(FP8X4),
+                scales=xn_scales[:, t, js].rearrange("q j g p -> q (j g p)"),
+                in_=xn_grouped[pair, t][:].rearrange("q j g p v -> q (j g p v)"),
+            )
+
+        def regroup_x(engine_copy, h, t, nodes=slice(0, QUARTER)):
+            engine_copy(
+                out=xc_grouped[h][:, t, nodes], in_=x_raw[h][:].rearrange("p j (n t) -> p t n j", t=T)[:, t, nodes]
+            )
+
+        def quantise_channels(h, t):
+            nc.vector.quantize_mx(
+                out=xc_codes[:, t, quarter(h)].bitcast(FP8X4),
+                scales=xc_scales[:, t, quarter(h)],
+                in_=xc_grouped[h][:, t].rearrange("p n j -> p (n j)"),
+            )
+
+        def regroup_weights():
+            nc.vector.tensor_copy(out=w_grouped[:], in_=w_raw[:].rearrange("p k j o -> p k o j"))
+
+        def quantise_weights():
+            nc.vector.quantize_mx(
+                out=w_codes[:].rearrange("p k o -> p (k o)").bitcast(FP8X4),
+                scales=w_scales[:].rearrange("p k o -> p (k o)"),
+                in_=w_grouped[:].rearrange("p k o j -> p (k o j)"),
+            )
+
+        tx_grouped = {}
+
+        def tx1(b, t, tx):
+            for j in range(PACK):
+                for g in range(2):
+                    nc.tensor.matmul_mx(
+                        out=tx[:, j, :],
+                        lhsT=xn_codes[:, t, j, g, :].bitcast(FP8X4),
+                        lhsT_scale=xn_scales[:, t, j, g, :],
+                        rhs=s_codes[:, b // 2, g, block_of(b % 2)].bitcast(FP8X4),
+                        rhs_scale=s_scales[:, b // 2, g, block_of(b % 2)],
+                        start=(g == 0),
+                        stop=(g == 1),
+                    )
+            if b // 2 not in tx_grouped:
+                tx_grouped[b // 2] = stage.tile([P, T, 2 * P, PACK], BF16, name="tx_grouped", align_bytes=64)
+            nc.scalar.copy(
+                out=tx_grouped[b // 2][:, t, block_of(b % 2), :], in_=tx[:].rearrange("p j v -> p v j")
+            )
+
+        def quantise_tx(h, t, part):
+            nodes = slice(h * QUARTER + part.start, h * QUARTER + part.stop)
+            nc.vector.quantize_mx(
+                out=tx_codes[:, t, nodes].bitcast(FP8X4),
+                scales=tx_scales[:, t, nodes],
+                in_=tx_grouped[h][:, t, part].rearrange("p v j -> p (v j)"),
+            )
+
+        def result(b, both):
             for t in range(T):
-                nc.vector.tensor_copy(out=xc_grouped[:, t], in_=x_raw[h][:].rearrange("p j (n t) -> p t n j", t=T)[:, t])
+                for k, codes, scales in ((0, xc_codes, xc_scales), (1, tx_codes, tx_scales)):
+                    nc.tensor.matmul_mx(
+                        out=both[:, t, :],
+                        lhsT=codes[:, t, block_of(b)].bitcast(FP8X4),
+                        lhsT_scale=scales[:, t, block_of(b)],
+                        rhs=w_codes[:, k, :].bitcast(FP8X4),
+                        rhs_scale=w_scales[:, k, :],
+                        start=(k == 0),
+                        stop=(k == 1),
+                    )
+            rows = stage.tile([P, T, C_OUT], F32, name="rows", bufs=3)
+            nc.scalar.copy(out=rows[:], in_=both[:])
+            nc.sync.dma_start(out=out_rows[b], in_=rows[:])
+
+        vector_copy, scalar_copy = nc.vector.tensor_copy, nc.scalar.copy
+        for part in range(2):
             for t in range(T):
-                nc.vector.quantize_mx(
-                    out=xc_codes[:, t, h * QUARTER : (h + 1) * QUARTER].bitcast(FP8X4),
-                    scales=xc_scales[:, t, h * QUARTER : (h + 1) * QUARTER],
-                    in_=xc_grouped[:, t].rearrange("p n j -> p (n j)"),
-                )
+                regroup_x(vector_copy, 2, t, block_of(part))
+        for t in range(T):
+            quantise_channels(2, t)
+        banks = [bank(k) for k in range(PACK)]
+        for slot in UPPER:
+            sigmoid(slot, L)
+            fill_diagonal(sig[:, slot, block_of(slot)], 0.0)
+            turn_row(slot, UPPER, banks)
+            sigmoid(slot, R)
+        for slot in LOWER:
+            fill_diagonal(adj_of(slot)[:, block_of(slot)], -16384.0)
+        for i in range(2):
+            nc.gpsimd.tensor_tensor(
+                out=col_sums[:, i], in0=sig[:, 2 * i, columns(R)], in1=sig[:, 2 * i + 1, columns(R)], op=ALU.add
+            )
+        nc.gpsimd.tensor_tensor(out=col_sums[:, 2], in0=col_sums[:, 0], in1=col_sums[:, 1], op=ALU.add)
+        for slot in UPPER:
+            add(banks[slot], slot, L)
+        banks = [bank(PACK + k) for k in range(PACK)]
+        for slot in LOWER:
+            sigmoid(slot, L)
+            turn_row(slot, UPPER, banks)
+        for slot in UPPER:
+            add(banks[slot], slot, R)
+        banks = [bank(k) for k in range(PACK)]
+        for slot in LOWER:
+            sigmoid(slot, R)
+            turn_row(slot, LOWER, banks)
+        root_table = keep.tile([P, 1], F32)
+        nc.scalar.activation(out=root_table[:], in_=ident[:, 0:1], func=ACT.Sqrt)
+        add_column_sums(bank(4))
+        for slot in LOWER:
+            add(banks[slot - PACK], slot, R)
+        late = keep.tile([P, 2 * SLOTS * NODES], BF16, name="late", tag="sig", align_bytes=64)
+        XC = T * QUARTER * PACK
+        for i, h in enumerate((3, 0, 1)):
+            xc_grouped[h] = late[:, i * XC : (i + 1) * XC].rearrange("p (t n j) -> p t n j", t=T, j=PACK)
+        SG = 2 * QUARTER * PACK
+        for h in range(2):
+            first = 3 * XC + h * SG
+            s_grouped[h] = late[:, first : first + SG].rearrange("p (g w v) -> p g w v", g=2, v=PACK)
 
-        for i in range(AHEAD):
-            columns_of_s(QUARTER_ORDER[i])
+        steps = [(j, t) for pair in range(2) for t in range(T) for j in (2 * pair, 2 * pair + 1)]
+        x_numbers = [6, 7, 4, 5, 0, 1, 2, 6, 7, 4, 5, 0]
+        x_banks = {}
 
-        w_grouped = keep.tile([P, 2, C_OUT, PACK], BF16, align_bytes=64)
-        w_codes = keep.tile([P, 2, C_OUT], U32, align_bytes=64)
-        w_scales = keep.tile([P, 2, C_OUT], U8, align_bytes=64)
-        nc.vector.tensor_copy(out=w_grouped[:], in_=w_raw[:].rearrange("p k j o -> p k o j"))
-        nc.vector.quantize_mx(
-            out=w_codes[:].rearrange("p k o -> p (k o)").bitcast(FP8X4),
-            scales=w_scales[:].rearrange("p k o -> p (k o)"),
-            in_=w_grouped[:].rearrange("p k o j -> p (k o j)"),
-        )
+        def x_turn_step(i):
+            x_banks[i] = bank(x_numbers[i], (P, SLOTS, P), BF16)
+            turn_x(*steps[i], x_banks[i])
 
-        def tx1_of_block(block):
-            tx_grouped = stage.tile([P, T, P, PACK], BF16, align_bytes=64, bufs=3)
-            for t in range(T):
-                tx = psum.tile([P, PACK, P], F32, tag="a")
-                for j in range(PACK):
-                    for g in range(2):
-                        nc.tensor.matmul_mx(
-                            out=tx[:, j, :],
-                            lhsT=xn_codes[:, g, t, j, :].bitcast(FP8X4),
-                            lhsT_scale=xn_scales[:, g, t, j, :],
-                            rhs=s_codes[:, g, block].bitcast(FP8X4),
-                            rhs_scale=s_scales[:, g, block],
-                            start=(g == 0),
-                            stop=(g == 1),
-                        )
-                nc.scalar.copy(out=tx_grouped[:, t], in_=tx[:].rearrange("p j v -> p v j"))
-                nc.vector.quantize_mx(
-                    out=tx_codes[:, t, block].bitcast(FP8X4),
-                    scales=tx_scales[:, t, block],
-                    in_=tx_grouped[:, t].rearrange("p v j -> p (v j)"),
-                )
+        def x_group_step(i):
+            group_x(*steps[i], x_banks[i])
 
-        def result_of_block(number, block):
-            both = psum.tile([P, T, C_OUT], F32, tag="b", bufs=3)
-            for t in range(T):
-                nc.tensor.matmul_mx(
-                    out=both[:, t, :],
-                    lhsT=xc_codes[:, t, block].bitcast(FP8X4),
-                    lhsT_scale=xc_scales[:, t, block],
-                    rhs=w_codes[:, 0, :].bitcast(FP8X4),
-                    rhs_scale=w_scales[:, 0, :],
-                    start=True,
-                    stop=False,
-                )
-                nc.tensor.matmul_mx(
-                    out=both[:, t, :],
-                    lhsT=tx_codes[:, t, block].bitcast(FP8X4),
-                    lhsT_scale=tx_scales[:, t, block],
-                    rhs=w_codes[:, 1, :].bitcast(FP8X4),
-                    rhs_scale=w_scales[:, 1, :],
-                    start=False,
-                    stop=True,
-                )
-            result = stage.tile([P, T, C_OUT], F32, bufs=3)
-            nc.scalar.copy(out=result[:], in_=both[:])
-            nc.sync.dma_start(out=out_rows[number], in_=result[:])
+        for i in range(7):
+            x_turn_step(i)
+        nc.vector.tensor_reduce(out=deg[:], in_=deg_parts[:], op=ALU.add, axis=AX.X)
+        nc.vector.reciprocal(out=inv_deg[:], in_=deg[:])
+        for i in range(4):
+            x_group_step(i)
+        nc.scalar.activation(out=inv_root[:], in_=inv_deg[:], func=ACT.Sqrt)
+        factors = {R: bank(3)}
+        spread(R, factors[R])
+        for v in UPPER:
+            scale_rows(nc.vector, sym_right, v, quarter(0))
+        for v in LOWER:
+            scale_rows(nc.gpsimd, sym_right, v, quarter(0))
+        for v in range(SLOTS):
+            scale_rows(nc.gpsimd, sym_right, v, quarter(1))
+        for v in UPPER:
+            scale_rows(nc.gpsimd, sym_left, v, slice(0, HALF))
+        for i in range(7, 12):
+            x_turn_step(i)
+            x_group_step(i - 3)
+        scale_columns(0, 2)
+        quantise_x(0, 0)
+        scale_columns(1, 2)
+        quantise_x(1, 0)
+        for i in range(9, 12):
+            x_group_step(i)
+        factors[L] = bank(0)
+        spread(L, factors[L])
+        quantise_s(2)
+        quantise_x(0, 1)
+        quantise_x(1, 1)
 
-        numbers = [2 * h + b for h in QUARTER_ORDER for b in range(2)]
-        blocks = [slice(number * P, (number + 1) * P) for number in numbers]
-        for i in range(len(numbers) + LAG):
-            if i < len(numbers):
-                if i % 2 == 0 and i // 2 + AHEAD < QUARTERS:
-                    columns_of_s(QUARTER_ORDER[i // 2 + AHEAD])
-                tx1_of_block(blocks[i])
-                if i % 2 == 0:
-                    x_over_channels(numbers[i] // 2)
-            if i >= LAG:
-                result_of_block(numbers[i - LAG], blocks[i - LAG])
+        pairs = (2, 3, 0, 1)
+        beside = [
+            lambda: quantise_x(0, 2),
+            lambda: quantise_x(1, 2),
+            lambda: scale_columns(0, 3),
+            regroup_weights,
+            lambda: scale_columns(1, 3),
+            lambda: quantise_s(3),
+            quantise_weights,
+            lambda: quantise_channels(3, 0),
+            lambda: scale_columns(0, 0),
+            lambda: quantise_channels(3, 1),
+            lambda: quantise_s(0),
+            lambda: quantise_channels(3, 2),
+            lambda: scale_columns(0, 1),
+            lambda: regroup_x(vector_copy, 0, 0),
+            lambda: regroup_x(vector_copy, 0, 1),
+            lambda: quantise_s(1),
+        ]
+        for h in (0, 1):
+            beside += [lambda h=h, t=t: regroup_x(vector_copy, h, t) for t in range(2 if h == 0 else 0, T)]
+            beside += [lambda h=h, t=t: quantise_channels(h, t) for t in range(T)]
+        tx_numbers = [1, 2, 4, 5]
+        both_numbers = [6, 7]
+        count = mirrors = 0
+        for i, h in enumerate(pairs):
+            last = i == len(pairs) - 1
+            order = [(b, t) for b in range(2) for t in range(T)] if last else [(b, t) for t in range(T) for b in range(2)]
+            for step, (b, t) in enumerate(order):
+                tx1(2 * h + b, t, bank(tx_numbers[count % 4]))
+                count += 1
+                if i == 0 and step % 2 == 1:
+                    regroup_x(scalar_copy, 3, step // 2)
+                if (i, step) in ((0, 4), (0, 5), (1, 0), (1, 1)):
+                    k = mirrors
+                    mirror(k, bank(6 + k % 2, (P, PACK, P), BF16))
+                    mirrors += 1
+                for k in range(2 if i == 0 and step < 4 else 1):
+                    if beside:
+                        beside.pop(0)()
+                if last:
+                    quantise_tx(h, t, block_of(b))
+                elif b == 1:
+                    quantise_tx(h, t, slice(0, QUARTER))
+                if i > 0 and step in ((1, 3) if last else (3, 5)):
+                    k = step // 3 if last else step // 4
+                    result(2 * pairs[i - 1] + k, bank(both_numbers[k], (P, T, C_OUT)))
+                if last and step == 4:
+                    result(2 * h, bank(both_numbers[0], (P, T, C_OUT)))
+        result(2 * pairs[-1] + 1, bank(both_numbers[1], (P, T, C_OUT)))

@@ -72,7 +72,6 @@ def tile_dynamicgraphspatialconv_pa_kernel(tc, x, adj_param, w_cheb0, w_cheb1, o
         sig = keep.tile([P, SLOTS, NODES], F32, name="sig", tag="sig", align_bytes=64)
         sym_right = keep.tile([P, SLOTS, HALF], F32)
         sym_left = keep.tile([P, PACK, HALF], F32)
-        col_sums = keep.tile([P, 3, HALF], F32)
         xn_codes = keep.tile([P, T, PACK, 2, P], U32, align_bytes=64)
         xn_scales = keep.tile([P, T, PACK, 2, P], U8, align_bytes=64)
         xc_codes = keep.tile([P, T, NODES], U32, align_bytes=64)
@@ -141,16 +140,20 @@ def tile_dynamicgraphspatialconv_pa_kernel(tc, x, adj_param, w_cheb0, w_cheb1, o
                 accum_out=deg_parts[:, slot, column : column + 1],
             )
 
-        def add_column_sums(turned):
-            unused = stage.tile([P, PACK, P], F32, name="unused", bufs=1)
-            for k in range(PACK):
-                nc.tensor.transpose(turned[:, k, :], col_sums[:, 2, block_of(k)], ident[:])
-            for k in range(PACK):
+        def turn_adjacency(i, turned):
+            for k in range(2):
+                for slot in UPPER:
+                    block = adj_of(slot)[:, block_of(PACK + 2 * i + k)]
+                    nc.tensor.transpose(turned[:, k, slot, :], block, ident_bf[:])
+
+        def add_column_sums(i, turned):
+            for k in range(2):
+                unused = stage.tile([P, HALF], F32, name="unused")
                 nc.scalar.activation(
-                    out=unused[:, k],
-                    in_=turned[:, k, :],
-                    func=ACT.Copy,
-                    accum_out=deg_parts[:, PACK + k, 2:3],
+                    out=unused[:],
+                    in_=turned[:, k].rearrange("q s w -> q (s w)"),
+                    func=ACT.Sigmoid,
+                    accum_out=deg_parts[:, PACK + 2 * i + k, 2:3],
                 )
 
         def spread(half, along_free):
@@ -297,6 +300,7 @@ def tile_dynamicgraphspatialconv_pa_kernel(tc, x, adj_param, w_cheb0, w_cheb1, o
                 regroup_x(vector_copy, 2, t, block_of(part))
         for t in range(T):
             quantise_channels(2, t)
+        turned_adjacency = {}
         banks = [bank(k) for k in range(PACK)]
         for slot in UPPER:
             sigmoid(slot, L)
@@ -305,11 +309,6 @@ def tile_dynamicgraphspatialconv_pa_kernel(tc, x, adj_param, w_cheb0, w_cheb1, o
             sigmoid(slot, R)
         for slot in LOWER:
             fill_diagonal(adj_of(slot)[:, block_of(slot)], -16384.0)
-        for i in range(2):
-            nc.gpsimd.tensor_tensor(
-                out=col_sums[:, i], in0=sig[:, 2 * i, columns(R)], in1=sig[:, 2 * i + 1, columns(R)], op=ALU.add
-            )
-        nc.gpsimd.tensor_tensor(out=col_sums[:, 2], in0=col_sums[:, 0], in1=col_sums[:, 1], op=ALU.add)
         for slot in UPPER:
             add(banks[slot], slot, L)
         banks = [bank(PACK + k) for k in range(PACK)]
@@ -322,9 +321,14 @@ def tile_dynamicgraphspatialconv_pa_kernel(tc, x, adj_param, w_cheb0, w_cheb1, o
         for slot in LOWER:
             sigmoid(slot, R)
             turn_row(slot, LOWER, banks)
+            if slot in (PACK + 1, PACK + 2):
+                i = slot - PACK - 1
+                turned_adjacency[i] = bank(PACK + i, (P, 2, PACK, P), BF16)
+                turn_adjacency(i, turned_adjacency[i])
+        for i in range(2):
+            add_column_sums(i, turned_adjacency[i])
         root_table = keep.tile([P, 1], F32)
         nc.scalar.activation(out=root_table[:], in_=ident[:, 0:1], func=ACT.Sqrt)
-        add_column_sums(bank(4))
         for slot in LOWER:
             add(banks[slot - PACK], slot, R)
         late = keep.tile([P, 2 * SLOTS * NODES], BF16, name="late", tag="sig", align_bytes=64)
@@ -347,15 +351,16 @@ def tile_dynamicgraphspatialconv_pa_kernel(tc, x, adj_param, w_cheb0, w_cheb1, o
         def x_group_step(i):
             group_x(*steps[i], x_banks[i])
 
-        for i in range(7):
+        for i in range(6):
             x_turn_step(i)
         nc.vector.tensor_reduce(out=deg[:], in_=deg_parts[:], op=ALU.add, axis=AX.X)
         nc.vector.reciprocal(out=inv_deg[:], in_=deg[:])
-        for i in range(4):
-            x_group_step(i)
         nc.scalar.activation(out=inv_root[:], in_=inv_deg[:], func=ACT.Sqrt)
         factors = {R: bank(3)}
         spread(R, factors[R])
+        x_turn_step(6)
+        for i in range(4):
+            x_group_step(i)
         for v in UPPER:
             scale_rows(nc.vector, sym_right, v, quarter(0))
         for v in LOWER:

@@ -36,31 +36,32 @@ def tile_dynamicgraphspatialconv_pa_kernel(tc, x, adj_param, w_cheb0, w_cheb1, o
         psum = stack.enter_context(tc.psum_pool(name="psum", bufs=1))
         stack.enter_context(tc.manual_schedule())
 
-        adj_rows = adj_param.rearrange("(s q) m -> s q m", q=P)
+        adj_rows = adj_param.rearrange("(k c q) m -> c k q m", k=PACK, c=2)
         adj_sb = [keep.tile([P, 2, NODES], BF16, name="adj%d" % i, tag="adj%d" % i, align_bytes=64) for i in range(PACK)]
 
         def adj_of(slot):
             return adj_sb[slot // 2][:, slot % 2]
 
-        for half in range(2):
-            cols = slice(half * HALF, (half + 1) * HALF)
-            nc.sync.dma_start(out=adj_of(0)[:, cols], in_=adj_rows[0][:, cols])
-        x_rows = x[0].rearrange("(p j) (h n) t -> h p j (n t)", j=PACK, h=QUARTERS)
+        x_rows = x[0].rearrange("(p j) (k c n) t -> c k p j (n t)", j=PACK, k=PACK, c=2)
         x_raw = [keep.tile([P, PACK, QUARTER * T], BF16, name="xraw%d" % h) for h in range(QUARTERS)]
-        for slot in range(1, SLOTS):
-            nc.sync.dma_start(out=adj_of(slot), in_=adj_rows[slot])
-            if slot < 3:
-                cols = slice((slot - 1) * P * T, slot * P * T)
-                nc.sync.dma_start(out=x_raw[2][:, :, cols], in_=x_rows[2][:, :, cols])
-        x_turn_rows = x[0].rearrange("(j G e) (s n) t -> j (e s) G (n t)", j=PACK, e=16, s=SLOTS)
-        x_turn = [keep.tile([P, SLOTS, P * T], BF16, name="xturn%d" % j) for j in range(PACK)]
+
+        def load_x(slot):
+            cols = slice((slot % 2) * P * T, (slot % 2 + 1) * P * T)
+            nc.sync.dma_start(out=x_raw[slot // 2][:, :, cols], in_=x_rows[slot // PACK][slot % PACK])
+
+        for slot in range(SLOTS):
+            nc.sync.dma_start(out=adj_of(slot), in_=adj_rows[slot // PACK][slot % PACK])
+            if slot in (1, 2):
+                load_x(PACK + slot - 1)
+        x_turn_rows = x[0].rearrange("(j G e) (k n) t -> j (e k) G (n t)", j=PACK, G=PACK, k=PACK)
+        x_turn = [keep.tile([P, PACK, QUARTER * T], BF16, name="xturn%d" % j) for j in range(PACK)]
         for j in range(PACK):
             nc.sync.dma_start(out=x_turn[j][:], in_=x_turn_rows[j])
         w_raw = keep.tile([P, 2, PACK, C_OUT], BF16)
         nc.sync.dma_start(out=w_raw[:, 0], in_=w_cheb0.rearrange("(p j) o -> p j o", j=PACK))
         nc.sync.dma_start(out=w_raw[:, 1], in_=w_cheb1.rearrange("(j p) o -> p j o", j=PACK))
-        for h in (3, 0, 1):
-            nc.sync.dma_start(out=x_raw[h][:], in_=x_rows[h])
+        for slot in (6, 7, 0, 1, 2, 3):
+            load_x(slot)
 
         ident = keep.tile([P, P], F32)
         make_identity(nc, ident[:])
@@ -87,7 +88,7 @@ def tile_dynamicgraphspatialconv_pa_kernel(tc, x, adj_param, w_cheb0, w_cheb1, o
         w_grouped = keep.tile([P, 2, C_OUT, PACK], BF16, align_bytes=64)
         w_codes = keep.tile([P, 2, C_OUT], U32, align_bytes=64)
         w_scales = keep.tile([P, 2, C_OUT], U8, align_bytes=64)
-        out_rows = out[0].rearrange("t (b q) o -> b q t o", q=P)
+        out_rows = out[0].rearrange("t (k c q) o -> c k q t o", k=PACK, c=2)
 
         xc_early = keep.tile([P, T, QUARTER, PACK], BF16, align_bytes=64)
         xc_grouped = {2: xc_early}
@@ -106,8 +107,8 @@ def tile_dynamicgraphspatialconv_pa_kernel(tc, x, adj_param, w_cheb0, w_cheb1, o
 
         def sigmoid(slot, half):
             nc.scalar.activation(
-                out=sig[:, slot, columns(half)],
-                in_=adj_of(slot)[:, columns(half)],
+                out=sig[:, slot, columns(half)].rearrange("q (k w) -> q k w", k=PACK),
+                in_=adj_of(slot).rearrange("q (k c w) -> q c k w", k=PACK, c=2)[:, half],
                 func=ACT.Sigmoid,
                 accum_out=(deg_parts[:, slot, 0:1] if (slot in LOWER and half == L) else None),
             )
@@ -143,7 +144,7 @@ def tile_dynamicgraphspatialconv_pa_kernel(tc, x, adj_param, w_cheb0, w_cheb1, o
         def turn_adjacency(i, turned):
             for k in range(2):
                 for slot in UPPER:
-                    block = adj_of(slot)[:, block_of(PACK + 2 * i + k)]
+                    block = adj_of(slot)[:, block_of(2 * (2 * i + k) + 1)]
                     nc.tensor.transpose(turned[:, k, slot, :], block, ident_bf[:])
 
         def add_column_sums(i, turned):
@@ -203,12 +204,13 @@ def tile_dynamicgraphspatialconv_pa_kernel(tc, x, adj_param, w_cheb0, w_cheb1, o
         xn_grouped = {}
 
         def turn_x(j, t, turned):
-            for G in range(SLOTS):
-                block = x_turn[j][:, G, :].rearrange("p (n t) -> p t n", t=T)[:, t, :]
-                if G % 2 == 0:
-                    nc.tensor.matmul(turned[:, G, :], lhsT=block, rhs=ident_bf[:], start=True, stop=True)
+            for i in range(2 * PACK):
+                g, G = i // PACK, i % PACK
+                block = x_turn[j][:, G, :].rearrange("p (g n t) -> p g t n", g=2, t=T)[:, g, t, :]
+                if i % 2 == 0:
+                    nc.tensor.matmul(turned[:, i, :], lhsT=block, rhs=ident_bf[:], start=True, stop=True)
                 else:
-                    nc.tensor.transpose(turned[:, G, :], block, ident_bf[:])
+                    nc.tensor.transpose(turned[:, i, :], block, ident_bf[:])
 
         def group_x(j, t, turned):
             if j % 2 == 0:
@@ -216,8 +218,8 @@ def tile_dynamicgraphspatialconv_pa_kernel(tc, x, adj_param, w_cheb0, w_cheb1, o
                 tag = "adj%d" % i if i < PACK else "xn%d" % i
                 xn_grouped[j // 2, t] = keep.tile([P, 2, 2, P, PACK], BF16, name="xn%d" % i, tag=tag, align_bytes=64)
             nc.scalar.copy(
-                out=xn_grouped[j // 2, t][:, j % 2].rearrange("q g c v -> q g (c v)").bitcast(F32),
-                in_=turned[:].rearrange("q G c -> q (G c)").bitcast(F32).rearrange("q (c g w) -> q g c w", g=2, w=2),
+                out=xn_grouped[j // 2, t][:, j % 2].rearrange("q g c v -> q (g c v)").bitcast(F32),
+                in_=turned[:].rearrange("q i c -> q (i c)").bitcast(F32),
             )
 
         def quantise_x(pair, t):
@@ -292,9 +294,9 @@ def tile_dynamicgraphspatialconv_pa_kernel(tc, x, adj_param, w_cheb0, w_cheb1, o
                     )
             rows = stage.tile([P, T, C_OUT], F32, name="rows", bufs=3)
             nc.scalar.copy(out=rows[:], in_=both[:])
-            nc.sync.dma_start(out=out_rows[b], in_=rows[:])
+            nc.sync.dma_start(out=out_rows[b // PACK][b % PACK], in_=rows[:])
 
-        vector_copy, scalar_copy = nc.vector.tensor_copy, nc.scalar.copy
+        vector_copy = nc.vector.tensor_copy
         for part in range(2):
             for t in range(T):
                 regroup_x(vector_copy, 2, t, block_of(part))
@@ -308,7 +310,7 @@ def tile_dynamicgraphspatialconv_pa_kernel(tc, x, adj_param, w_cheb0, w_cheb1, o
             turn_row(slot, UPPER, banks)
             sigmoid(slot, R)
         for slot in LOWER:
-            fill_diagonal(adj_of(slot)[:, block_of(slot)], -16384.0)
+            fill_diagonal(adj_of(slot)[:, block_of(2 * (slot % PACK) + slot // PACK)], -16384.0)
         for slot in UPPER:
             add(banks[slot], slot, L)
         banks = [bank(PACK + k) for k in range(PACK)]
@@ -340,7 +342,7 @@ def tile_dynamicgraphspatialconv_pa_kernel(tc, x, adj_param, w_cheb0, w_cheb1, o
             first = 3 * XC + h * SG
             s_grouped[h] = late[:, first : first + SG].rearrange("p (g w v) -> p g w v", g=2, v=PACK)
 
-        steps = [(j, t) for pair in range(2) for t in range(T) for j in (2 * pair, 2 * pair + 1)]
+        steps = [(j, t) for j in range(PACK) for t in range(T)]
         x_numbers = [6, 7, 4, 5, 0, 1, 2, 6, 7, 4, 5, 0]
         x_banks = {}
 
@@ -355,11 +357,12 @@ def tile_dynamicgraphspatialconv_pa_kernel(tc, x, adj_param, w_cheb0, w_cheb1, o
             x_turn_step(i)
         nc.vector.tensor_reduce(out=deg[:], in_=deg_parts[:], op=ALU.add, axis=AX.X)
         nc.vector.reciprocal(out=inv_deg[:], in_=deg[:])
+        x_group_step(0)
         nc.scalar.activation(out=inv_root[:], in_=inv_deg[:], func=ACT.Sqrt)
         factors = {R: bank(3)}
         spread(R, factors[R])
         x_turn_step(6)
-        for i in range(4):
+        for i in range(1, 4):
             x_group_step(i)
         for v in UPPER:
             scale_rows(nc.vector, sym_right, v, quarter(0))
@@ -375,37 +378,37 @@ def tile_dynamicgraphspatialconv_pa_kernel(tc, x, adj_param, w_cheb0, w_cheb1, o
         scale_columns(0, 2)
         quantise_x(0, 0)
         scale_columns(1, 2)
-        quantise_x(1, 0)
+        quantise_x(0, 1)
         for i in range(9, 12):
             x_group_step(i)
-        factors[L] = bank(0)
-        spread(L, factors[L])
         quantise_s(2)
-        quantise_x(0, 1)
+        quantise_x(1, 0)
         quantise_x(1, 1)
 
         pairs = (2, 3, 0, 1)
         beside = [
             lambda: quantise_x(0, 2),
-            lambda: quantise_x(1, 2),
             lambda: scale_columns(0, 3),
-            regroup_weights,
+            lambda: quantise_x(1, 2),
             lambda: scale_columns(1, 3),
+            regroup_weights,
             lambda: quantise_s(3),
             quantise_weights,
-            lambda: quantise_channels(3, 0),
             lambda: scale_columns(0, 0),
+            lambda: quantise_channels(3, 0),
             lambda: quantise_channels(3, 1),
+            lambda: scale_columns(0, 1),
             lambda: quantise_s(0),
             lambda: quantise_channels(3, 2),
-            lambda: scale_columns(0, 1),
             lambda: regroup_x(vector_copy, 0, 0),
-            lambda: regroup_x(vector_copy, 0, 1),
             lambda: quantise_s(1),
         ]
-        for h in (0, 1):
-            beside += [lambda h=h, t=t: regroup_x(vector_copy, h, t) for t in range(2 if h == 0 else 0, T)]
-            beside += [lambda h=h, t=t: quantise_channels(h, t) for t in range(T)]
+        beside += [lambda t=t: regroup_x(vector_copy, 0, t) for t in (1, 2)]
+        beside += [lambda t=t: quantise_channels(0, t) for t in range(T)]
+        beside += [lambda t=t: regroup_x(vector_copy, 1, t) for t in range(T)]
+        beside += [lambda t=t: quantise_channels(1, t) for t in range(T)]
+        POPS = ((2, 1, 2, 1, 1, 1), (1, 2, 1, 1, 1, 1), (2, 2, 1, 2, 1, 1), (1, 1, 0, 0, 0, 0))
+        MIRRORS = ((0, 4), (0, 5), (1, 0), (1, 1))
         tx_numbers = [1, 2, 4, 5]
         both_numbers = [6, 7]
         count = mirrors = 0
@@ -415,22 +418,24 @@ def tile_dynamicgraphspatialconv_pa_kernel(tc, x, adj_param, w_cheb0, w_cheb1, o
             for step, (b, t) in enumerate(order):
                 tx1(2 * h + b, t, bank(tx_numbers[count % 4]))
                 count += 1
+                if i == 0 and step == 2:
+                    factors[L] = bank(0)
+                    spread(L, factors[L])
                 if i == 0 and step % 2 == 1:
-                    regroup_x(scalar_copy, 3, step // 2)
-                if (i, step) in ((0, 4), (0, 5), (1, 0), (1, 1)):
+                    regroup_x(nc.scalar.copy, 3, step // 2)
+                if (i, step) in MIRRORS:
                     k = mirrors
                     mirror(k, bank(6 + k % 2, (P, PACK, P), BF16))
                     mirrors += 1
-                for k in range(2 if i == 0 and step < 4 else 1):
+                for k in range(POPS[i][step]):
                     if beside:
                         beside.pop(0)()
                 if last:
                     quantise_tx(h, t, block_of(b))
                 elif b == 1:
                     quantise_tx(h, t, slice(0, QUARTER))
-                if i > 0 and step in ((1, 3) if last else (3, 5)):
-                    k = step // 3 if last else step // 4
+                if i > 0 and step in ((4, 5) if last else (3, 5)):
+                    k = step - 4 if last else step // 4
                     result(2 * pairs[i - 1] + k, bank(both_numbers[k], (P, T, C_OUT)))
-                if last and step == 4:
-                    result(2 * h, bank(both_numbers[0], (P, T, C_OUT)))
+        result(2 * pairs[-1], bank(both_numbers[0], (P, T, C_OUT)))
         result(2 * pairs[-1] + 1, bank(both_numbers[1], (P, T, C_OUT)))

@@ -49,7 +49,10 @@ def tile_dynamicgraphspatialconv_pa_kernel(tc, x, adj_param, w_cheb0, w_cheb1, o
             cols = slice((slot % 2) * P * T, (slot % 2 + 1) * P * T)
             nc.sync.dma_start(out=x_raw[slot // 2][:, :, cols], in_=x_rows[slot // PACK][slot % PACK])
 
-        for slot in range(SLOTS):
+        for half in range(2):
+            cols = slice(half * HALF, (half + 1) * HALF)
+            nc.sync.dma_start(out=adj_of(0)[:, cols], in_=adj_rows[0][0][:, cols])
+        for slot in range(1, SLOTS):
             nc.sync.dma_start(out=adj_of(slot), in_=adj_rows[slot // PACK][slot % PACK])
             if slot in (1, 2):
                 load_x(PACK + slot - 1)
@@ -112,6 +115,15 @@ def tile_dynamicgraphspatialconv_pa_kernel(tc, x, adj_param, w_cheb0, w_cheb1, o
                 func=ACT.Sigmoid,
                 accum_out=(deg_parts[:, slot, 0:1] if (slot in LOWER and half == L) else None),
             )
+
+        def first_sigmoids():
+            for i in range(2):
+                blocks = slice(2 * i, 2 * i + 2)
+                nc.scalar.activation(
+                    out=sig[:, 0].rearrange("q (c k w) -> q c k w", c=2, k=PACK)[:, :, blocks],
+                    in_=adj_of(0).rearrange("q (k c w) -> q c k w", k=PACK, c=2)[:, :, blocks],
+                    func=ACT.Sigmoid,
+                )
 
         def fill_diagonal(block, fill):
             nc.gpsimd.affine_select(
@@ -280,8 +292,8 @@ def tile_dynamicgraphspatialconv_pa_kernel(tc, x, adj_param, w_cheb0, w_cheb1, o
                 in_=tx_grouped[h][:, t, part].rearrange("p v j -> p (v j)"),
             )
 
-        def result(b, both):
-            for t in range(T):
+        def result(b, both, steps=range(T)):
+            for t in steps:
                 for k, codes, scales in ((0, xc_codes, xc_scales), (1, tx_codes, tx_scales)):
                     nc.tensor.matmul_mx(
                         out=both[:, t, :],
@@ -292,9 +304,10 @@ def tile_dynamicgraphspatialconv_pa_kernel(tc, x, adj_param, w_cheb0, w_cheb1, o
                         start=(k == 0),
                         stop=(k == 1),
                     )
-            rows = stage.tile([P, T, C_OUT], F32, name="rows", bufs=3)
-            nc.scalar.copy(out=rows[:], in_=both[:])
-            nc.sync.dma_start(out=out_rows[b // PACK][b % PACK], in_=rows[:])
+            part = slice(steps.start, steps.stop)
+            rows = stage.tile([P, T, C_OUT], F32, name="rows", bufs=5)
+            nc.scalar.copy(out=rows[:, part], in_=both[:, part])
+            nc.sync.dma_start(out=out_rows[b // PACK][b % PACK][:, part], in_=rows[:, part])
 
         vector_copy = nc.vector.tensor_copy
         for part in range(2):
@@ -305,10 +318,14 @@ def tile_dynamicgraphspatialconv_pa_kernel(tc, x, adj_param, w_cheb0, w_cheb1, o
         turned_adjacency = {}
         banks = [bank(k) for k in range(PACK)]
         for slot in UPPER:
-            sigmoid(slot, L)
+            if slot == 0:
+                first_sigmoids()
+            else:
+                sigmoid(slot, L)
             fill_diagonal(sig[:, slot, block_of(slot)], 0.0)
             turn_row(slot, UPPER, banks)
-            sigmoid(slot, R)
+            if slot > 0:
+                sigmoid(slot, R)
         for slot in LOWER:
             fill_diagonal(adj_of(slot)[:, block_of(2 * (slot % PACK) + slot // PACK)], -16384.0)
         for slot in UPPER:
@@ -367,11 +384,7 @@ def tile_dynamicgraphspatialconv_pa_kernel(tc, x, adj_param, w_cheb0, w_cheb1, o
         for v in UPPER:
             scale_rows(nc.vector, sym_right, v, quarter(0))
         for v in LOWER:
-            scale_rows(nc.gpsimd, sym_right, v, quarter(0))
-        for v in range(SLOTS):
-            scale_rows(nc.gpsimd, sym_right, v, quarter(1))
-        for v in UPPER:
-            scale_rows(nc.gpsimd, sym_left, v, slice(0, HALF))
+            scale_rows(nc.vector, sym_right, v, quarter(0))
         for i in range(7, 12):
             x_turn_step(i)
             x_group_step(i - 3)
@@ -381,33 +394,37 @@ def tile_dynamicgraphspatialconv_pa_kernel(tc, x, adj_param, w_cheb0, w_cheb1, o
         quantise_x(0, 1)
         for i in range(9, 12):
             x_group_step(i)
+        regroup_x(nc.scalar.copy, 3, 0)
         quantise_s(2)
         quantise_x(1, 0)
         quantise_x(1, 1)
 
         pairs = (2, 3, 0, 1)
+        def rows(table, cols, first, last):
+            for v in range(first, last):
+                scale_rows(nc.vector, table, v, cols)
+
         beside = [
-            lambda: quantise_x(0, 2),
+            lambda: (rows(sym_right, quarter(1), 0, PACK), quantise_x(0, 2)),
             lambda: scale_columns(0, 3),
-            lambda: quantise_x(1, 2),
+            lambda: (rows(sym_right, quarter(1), PACK, SLOTS), quantise_x(1, 2)),
             lambda: scale_columns(1, 3),
             regroup_weights,
             lambda: quantise_s(3),
-            quantise_weights,
-            lambda: scale_columns(0, 0),
+            lambda: (quantise_weights(), rows(sym_left, slice(0, HALF), 0, PACK)),
             lambda: quantise_channels(3, 0),
+            lambda: scale_columns(0, 0),
             lambda: quantise_channels(3, 1),
             lambda: scale_columns(0, 1),
             lambda: quantise_s(0),
             lambda: quantise_channels(3, 2),
-            lambda: regroup_x(vector_copy, 0, 0),
             lambda: quantise_s(1),
         ]
         beside += [lambda t=t: regroup_x(vector_copy, 0, t) for t in (1, 2)]
         beside += [lambda t=t: quantise_channels(0, t) for t in range(T)]
         beside += [lambda t=t: regroup_x(vector_copy, 1, t) for t in range(T)]
         beside += [lambda t=t: quantise_channels(1, t) for t in range(T)]
-        POPS = ((2, 1, 2, 1, 1, 1), (1, 2, 1, 1, 1, 1), (2, 2, 1, 2, 1, 1), (1, 1, 0, 0, 0, 0))
+        POPS = ((2, 1, 2, 1, 1, 1), (1, 2, 1, 1, 1, 0), (2, 2, 1, 2, 1, 1), (1, 1, 0, 0, 0, 0))
         MIRRORS = ((0, 4), (0, 5), (1, 0), (1, 1))
         tx_numbers = [1, 2, 4, 5]
         both_numbers = [6, 7]
@@ -421,8 +438,10 @@ def tile_dynamicgraphspatialconv_pa_kernel(tc, x, adj_param, w_cheb0, w_cheb1, o
                 if i == 0 and step == 2:
                     factors[L] = bank(0)
                     spread(L, factors[L])
-                if i == 0 and step % 2 == 1:
-                    regroup_x(nc.scalar.copy, 3, step // 2)
+                if i == 0 and step in (1, 3):
+                    regroup_x(nc.scalar.copy, 3, step // 2 + 1)
+                if (i, step) == (1, 2):
+                    regroup_x(nc.scalar.copy, 0, 0)
                 if (i, step) in MIRRORS:
                     k = mirrors
                     mirror(k, bank(6 + k % 2, (P, PACK, P), BF16))
@@ -438,4 +457,6 @@ def tile_dynamicgraphspatialconv_pa_kernel(tc, x, adj_param, w_cheb0, w_cheb1, o
                     k = step - 4 if last else step // 4
                     result(2 * pairs[i - 1] + k, bank(both_numbers[k], (P, T, C_OUT)))
         result(2 * pairs[-1], bank(both_numbers[0], (P, T, C_OUT)))
-        result(2 * pairs[-1] + 1, bank(both_numbers[1], (P, T, C_OUT)))
+        both = bank(both_numbers[1], (P, T, C_OUT))
+        result(2 * pairs[-1] + 1, both, range(2))
+        result(2 * pairs[-1] + 1, both, range(2, T))

@@ -70,6 +70,8 @@ def tile_dynamicgraphspatialconv_pa_kernel(tc, x, adj_param, w_cheb0, w_cheb1, o
         make_identity(nc, ident[:])
         ident_bf = keep.tile([P, P], BF16)
         make_identity(nc, ident_bf[:])
+        minus_diagonal = keep.tile([P, P], BF16)
+        nc.vector.tensor_scalar(out=minus_diagonal[:], in0=ident_bf[:], scalar1=-16384.0, scalar2=None, op0=ALU.mult)
         deg_parts = keep.tile([P, SLOTS, 3], F32)
         nc.vector.memset(deg_parts[:], 0.0)
 
@@ -78,12 +80,12 @@ def tile_dynamicgraphspatialconv_pa_kernel(tc, x, adj_param, w_cheb0, w_cheb1, o
         sym_left = keep.tile([P, PACK, HALF], F32)
         xn_codes = keep.tile([P, T, PACK, 2, P], U32, align_bytes=64)
         xn_scales = keep.tile([P, T, PACK, 2, P], U8, align_bytes=64)
-        xc_codes = keep.tile([P, T, NODES], U32, align_bytes=64)
-        xc_scales = keep.tile([P, T, NODES], U8, align_bytes=64)
+        xc_codes = keep.tile([P, QUARTERS, T, QUARTER], U32, align_bytes=64)
+        xc_scales = keep.tile([P, QUARTERS, T, QUARTER], U8, align_bytes=64)
         s_codes = keep.tile([P, QUARTERS, 2, QUARTER], U32, align_bytes=64)
         s_scales = keep.tile([P, QUARTERS, 2, QUARTER], U8, align_bytes=64)
-        tx_codes = keep.tile([P, T, NODES], U32, align_bytes=64)
-        tx_scales = keep.tile([P, T, NODES], U8, align_bytes=64)
+        tx_codes = keep.tile([P, QUARTERS, T, QUARTER], U32, align_bytes=64)
+        tx_scales = keep.tile([P, QUARTERS, T, QUARTER], U8, align_bytes=64)
         s_grouped = {h: keep.tile([P, 2, QUARTER, PACK], BF16, name="s%d" % h, align_bytes=64) for h in (2, 3)}
         inv_root = keep.tile([P, SLOTS], F32)
         deg = keep.tile([P, SLOTS], F32)
@@ -117,23 +119,23 @@ def tile_dynamicgraphspatialconv_pa_kernel(tc, x, adj_param, w_cheb0, w_cheb1, o
             )
 
         def first_sigmoids():
-            for i in range(2):
-                blocks = slice(2 * i, 2 * i + 2)
+            for halves, blocks in ((slice(R, R + 1), slice(0, 2)), (slice(L, L + 1), slice(0, 2)), (slice(L, R + 1), slice(2, 4))):
                 nc.scalar.activation(
-                    out=sig[:, 0].rearrange("q (c k w) -> q c k w", c=2, k=PACK)[:, :, blocks],
-                    in_=adj_of(0).rearrange("q (k c w) -> q c k w", k=PACK, c=2)[:, :, blocks],
+                    out=sig[:, 0].rearrange("q (c k w) -> q c k w", c=2, k=PACK)[:, halves, blocks],
+                    in_=adj_of(0).rearrange("q (k c w) -> q c k w", k=PACK, c=2)[:, halves, blocks],
                     func=ACT.Sigmoid,
                 )
 
-        def fill_diagonal(block, fill):
-            nc.gpsimd.affine_select(
-                out=block,
-                in_=block,
-                pattern=[[-1, P]],
-                compare_op=ALU.not_equal,
-                fill=fill,
-                base=0,
-                channel_multiplier=1,
+        def mask_diagonal(slots):
+            first = slots[0]
+            blocks = adj_sb[first // 2][:].rearrange("q s (b w) -> q (s b) w", w=P)
+            start = 8 * (first % 2) + 2 * (first % PACK) + first // PACK
+            diagonal = blocks[:, start : start + 10 * len(slots) - 9 : 10]
+            nc.vector.tensor_tensor(
+                out=diagonal,
+                in0=diagonal,
+                in1=minus_diagonal[:].unsqueeze(1).to_broadcast([P, len(slots), P]),
+                op=ALU.add,
             )
 
         def turn_row(slot, column_slots, banks):
@@ -153,11 +155,9 @@ def tile_dynamicgraphspatialconv_pa_kernel(tc, x, adj_param, w_cheb0, w_cheb1, o
                 accum_out=deg_parts[:, slot, column : column + 1],
             )
 
-        def turn_adjacency(i, turned):
-            for k in range(2):
-                for slot in UPPER:
-                    block = adj_of(slot)[:, block_of(2 * (2 * i + k) + 1)]
-                    nc.tensor.transpose(turned[:, k, slot, :], block, ident_bf[:])
+        def turn_adjacency(k, turned):
+            for slot in UPPER:
+                nc.tensor.transpose(turned[:, k % 2, slot, :], adj_of(slot)[:, block_of(2 * k + 1)], ident_bf[:])
 
         def add_column_sums(i, turned):
             for k in range(2):
@@ -247,11 +247,11 @@ def tile_dynamicgraphspatialconv_pa_kernel(tc, x, adj_param, w_cheb0, w_cheb1, o
                 out=xc_grouped[h][:, t, nodes], in_=x_raw[h][:].rearrange("p j (n t) -> p t n j", t=T)[:, t, nodes]
             )
 
-        def quantise_channels(h, t):
+        def quantise_channels(h, first, last):
             nc.vector.quantize_mx(
-                out=xc_codes[:, t, quarter(h)].bitcast(FP8X4),
-                scales=xc_scales[:, t, quarter(h)],
-                in_=xc_grouped[h][:, t].rearrange("p n j -> p (n j)"),
+                out=xc_codes[:, h, first:last].rearrange("p t n -> p (t n)").bitcast(FP8X4),
+                scales=xc_scales[:, h, first:last].rearrange("p t n -> p (t n)"),
+                in_=xc_grouped[h][:, first:last].rearrange("p t n j -> p (t n j)"),
             )
 
         def regroup_weights():
@@ -285,10 +285,9 @@ def tile_dynamicgraphspatialconv_pa_kernel(tc, x, adj_param, w_cheb0, w_cheb1, o
             )
 
         def quantise_tx(h, t, part):
-            nodes = slice(h * QUARTER + part.start, h * QUARTER + part.stop)
             nc.vector.quantize_mx(
-                out=tx_codes[:, t, nodes].bitcast(FP8X4),
-                scales=tx_scales[:, t, nodes],
+                out=tx_codes[:, h, t, part].bitcast(FP8X4),
+                scales=tx_scales[:, h, t, part],
                 in_=tx_grouped[h][:, t, part].rearrange("p v j -> p (v j)"),
             )
 
@@ -297,8 +296,8 @@ def tile_dynamicgraphspatialconv_pa_kernel(tc, x, adj_param, w_cheb0, w_cheb1, o
                 for k, codes, scales in ((0, xc_codes, xc_scales), (1, tx_codes, tx_scales)):
                     nc.tensor.matmul_mx(
                         out=both[:, t, :],
-                        lhsT=codes[:, t, block_of(b)].bitcast(FP8X4),
-                        lhsT_scale=scales[:, t, block_of(b)],
+                        lhsT=codes[:, b // 2, t, block_of(b % 2)].bitcast(FP8X4),
+                        lhsT_scale=scales[:, b // 2, t, block_of(b % 2)],
                         rhs=w_codes[:, k, :].bitcast(FP8X4),
                         rhs_scale=w_scales[:, k, :],
                         start=(k == 0),
@@ -310,26 +309,29 @@ def tile_dynamicgraphspatialconv_pa_kernel(tc, x, adj_param, w_cheb0, w_cheb1, o
             nc.sync.dma_start(out=out_rows[b // PACK][b % PACK][:, part], in_=rows[:, part])
 
         vector_copy = nc.vector.tensor_copy
+        mask_diagonal((0,))
+        mask_diagonal((1,))
         for part in range(2):
             for t in range(T):
                 regroup_x(vector_copy, 2, t, block_of(part))
-        for t in range(T):
-            quantise_channels(2, t)
+                if t == part:
+                    mask_diagonal((2 + part,))
+        quantise_channels(2, 0, 2)
+        mask_diagonal((PACK, PACK + 1))
+        quantise_channels(2, 2, 3)
         turned_adjacency = {}
         banks = [bank(k) for k in range(PACK)]
         for slot in UPPER:
             if slot == 0:
                 first_sigmoids()
             else:
-                sigmoid(slot, L)
-            fill_diagonal(sig[:, slot, block_of(slot)], 0.0)
-            turn_row(slot, UPPER, banks)
-            if slot > 0:
                 sigmoid(slot, R)
-        for slot in LOWER:
-            fill_diagonal(adj_of(slot)[:, block_of(2 * (slot % PACK) + slot // PACK)], -16384.0)
+                sigmoid(slot, L)
+            turn_row(slot, UPPER, banks)
         for slot in UPPER:
             add(banks[slot], slot, L)
+            if slot == 0:
+                mask_diagonal((PACK + 2, PACK + 3))
         banks = [bank(PACK + k) for k in range(PACK)]
         for slot in LOWER:
             sigmoid(slot, L)
@@ -343,7 +345,8 @@ def tile_dynamicgraphspatialconv_pa_kernel(tc, x, adj_param, w_cheb0, w_cheb1, o
             if slot in (PACK + 1, PACK + 2):
                 i = slot - PACK - 1
                 turned_adjacency[i] = bank(PACK + i, (P, 2, PACK, P), BF16)
-                turn_adjacency(i, turned_adjacency[i])
+                for k in (2 * i, 2 * i + 1):
+                    turn_adjacency(k, turned_adjacency[i])
         for i in range(2):
             add_column_sums(i, turned_adjacency[i])
         root_table = keep.tile([P, 1], F32)
@@ -381,10 +384,8 @@ def tile_dynamicgraphspatialconv_pa_kernel(tc, x, adj_param, w_cheb0, w_cheb1, o
         x_turn_step(6)
         for i in range(1, 4):
             x_group_step(i)
-        for v in UPPER:
-            scale_rows(nc.vector, sym_right, v, quarter(0))
-        for v in LOWER:
-            scale_rows(nc.vector, sym_right, v, quarter(0))
+        for v in range(SLOTS):
+            scale_rows(nc.vector, sym_right, v, slice(0, HALF))
         for i in range(7, 12):
             x_turn_step(i)
             x_group_step(i - 3)
@@ -400,31 +401,36 @@ def tile_dynamicgraphspatialconv_pa_kernel(tc, x, adj_param, w_cheb0, w_cheb1, o
         quantise_x(1, 1)
 
         pairs = (2, 3, 0, 1)
-        def rows(table, cols, first, last):
-            for v in range(first, last):
-                scale_rows(nc.vector, table, v, cols)
+        def left_rows():
+            for v in UPPER:
+                scale_rows(nc.vector, sym_left, v, slice(0, HALF))
 
         beside = [
-            lambda: (rows(sym_right, quarter(1), 0, PACK), quantise_x(0, 2)),
+            lambda: quantise_x(0, 2),
             lambda: scale_columns(0, 3),
-            lambda: (rows(sym_right, quarter(1), PACK, SLOTS), quantise_x(1, 2)),
+            lambda: quantise_x(1, 2),
             lambda: scale_columns(1, 3),
             regroup_weights,
             lambda: quantise_s(3),
-            lambda: (quantise_weights(), rows(sym_left, slice(0, HALF), 0, PACK)),
-            lambda: quantise_channels(3, 0),
+            lambda: (quantise_weights(), left_rows()),
+            lambda: quantise_channels(3, 0, 2),
             lambda: scale_columns(0, 0),
-            lambda: quantise_channels(3, 1),
             lambda: scale_columns(0, 1),
             lambda: quantise_s(0),
-            lambda: quantise_channels(3, 2),
+            lambda: quantise_channels(3, 2, 3),
             lambda: quantise_s(1),
+            lambda: regroup_x(vector_copy, 0, 0),
+            lambda: regroup_x(vector_copy, 0, 1),
+            lambda: regroup_x(vector_copy, 0, 2),
+            lambda: quantise_channels(0, 0, 2),
+            lambda: quantise_channels(0, 2, 3),
+            lambda: regroup_x(vector_copy, 1, 0),
+            lambda: regroup_x(vector_copy, 1, 1),
+            lambda: regroup_x(vector_copy, 1, 2),
+            lambda: quantise_channels(1, 0, 2),
+            lambda: quantise_channels(1, 2, 3),
         ]
-        beside += [lambda t=t: regroup_x(vector_copy, 0, t) for t in (1, 2)]
-        beside += [lambda t=t: quantise_channels(0, t) for t in range(T)]
-        beside += [lambda t=t: regroup_x(vector_copy, 1, t) for t in range(T)]
-        beside += [lambda t=t: quantise_channels(1, t) for t in range(T)]
-        POPS = ((2, 1, 2, 1, 1, 1), (1, 2, 1, 1, 1, 0), (2, 2, 1, 2, 1, 1), (1, 1, 0, 0, 0, 0))
+        POPS = ((2, 1, 2, 1, 1, 1), (1, 1, 1, 1, 1, 1), (1, 1, 1, 1, 1, 1), (2, 1, 0, 0, 0, 0))
         MIRRORS = ((0, 4), (0, 5), (1, 0), (1, 1))
         tx_numbers = [1, 2, 4, 5]
         both_numbers = [6, 7]
@@ -440,8 +446,6 @@ def tile_dynamicgraphspatialconv_pa_kernel(tc, x, adj_param, w_cheb0, w_cheb1, o
                     spread(L, factors[L])
                 if i == 0 and step in (1, 3):
                     regroup_x(nc.scalar.copy, 3, step // 2 + 1)
-                if (i, step) == (1, 2):
-                    regroup_x(nc.scalar.copy, 0, 0)
                 if (i, step) in MIRRORS:
                     k = mirrors
                     mirror(k, bank(6 + k % 2, (P, PACK, P), BF16))

@@ -244,7 +244,8 @@ def tile_dynamicgraphspatialconv_pa_kernel(tc, x, adj_param, w_cheb0, w_cheb1, o
 
         def regroup_x(engine_copy, h, t, nodes=slice(0, QUARTER)):
             engine_copy(
-                out=xc_grouped[h][:, t, nodes], in_=x_raw[h][:].rearrange("p j (n t) -> p t n j", t=T)[:, t, nodes]
+                out=xc_grouped[h][:, t, nodes].rearrange("p (c i) j -> p c j i", i=PACK),
+                in_=x_raw[h][:].rearrange("p j (c i t) -> p t c j i", i=PACK, t=T)[:, t, nodes.start // PACK : nodes.stop // PACK],
             )
 
         def quantise_channels(h, first, last):

@@ -56,14 +56,16 @@ def tile_dynamicgraphspatialconv_pa_kernel(tc, x, adj_param, w_cheb0, w_cheb1, o
             nc.sync.dma_start(out=adj_of(slot), in_=adj_rows[slot // PACK][slot % PACK])
             if slot in (1, 2):
                 load_x(PACK + slot - 1)
+        for slot in (6, 7):
+            load_x(slot)
+        w_raw = keep.tile([P, 2, PACK, C_OUT], BF16)
+        nc.sync.dma_start(out=w_raw[:, 0], in_=w_cheb0.rearrange("(p j) o -> p j o", j=PACK))
+        nc.sync.dma_start(out=w_raw[:, 1], in_=w_cheb1.rearrange("(j p) o -> p j o", j=PACK))
         x_turn_rows = x[0].rearrange("(j G e) (k n) t -> j (e k) G (n t)", j=PACK, G=PACK, k=PACK)
         x_turn = [keep.tile([P, PACK, QUARTER * T], BF16, name="xturn%d" % j) for j in range(PACK)]
         for j in range(PACK):
             nc.sync.dma_start(out=x_turn[j][:], in_=x_turn_rows[j])
-        w_raw = keep.tile([P, 2, PACK, C_OUT], BF16)
-        nc.sync.dma_start(out=w_raw[:, 0], in_=w_cheb0.rearrange("(p j) o -> p j o", j=PACK))
-        nc.sync.dma_start(out=w_raw[:, 1], in_=w_cheb1.rearrange("(j p) o -> p j o", j=PACK))
-        for slot in (6, 7, 0, 1, 2, 3):
+        for slot in range(PACK):
             load_x(slot)
 
         ident = keep.tile([P, P], F32)
@@ -96,7 +98,7 @@ def tile_dynamicgraphspatialconv_pa_kernel(tc, x, adj_param, w_cheb0, w_cheb1, o
         out_rows = out[0].rearrange("t (k c q) o -> c k q t o", k=PACK, c=2)
 
         xc_early = keep.tile([P, T, QUARTER, PACK], BF16, align_bytes=64)
-        xc_grouped = {2: xc_early}
+        xc_grouped = {2: xc_early, 3: xc_early}
 
         def bank(number, shape=(P, PACK, P), dtype=F32):
             return psum.tile(list(shape), dtype, name="bank%d" % number, tag="bank%d" % number)
@@ -204,13 +206,14 @@ def tile_dynamicgraphspatialconv_pa_kernel(tc, x, adj_param, w_cheb0, w_cheb1, o
                 in_=s_grouped[h][:].rearrange("q g w v -> q (g w v)"),
             )
 
-        def mirror(b, mirrored):
-            for k in range(PACK):
-                upper = s_grouped[2 + k // 2][:, 0, (k % 2) * P : (k % 2 + 1) * P, b]
-                nc.tensor.transpose(mirrored[:, k, :], upper, ident_bf[:])
+        def mirror(h, mirrored):
+            for b in range(2):
+                for k in range(PACK):
+                    upper = s_grouped[2 + k // 2][:, 0, (k % 2) * P : (k % 2 + 1) * P, 2 * h + b]
+                    nc.tensor.transpose(mirrored[:, b, k, :], upper, ident_bf[:])
             nc.scalar.copy(
-                out=s_grouped[b // 2][:, 1, (b % 2) * P : (b % 2 + 1) * P, :],
-                in_=mirrored[:].rearrange("w k q -> w q k"),
+                out=s_grouped[h][:, 1].rearrange("w (b q) k -> w b q k", b=2),
+                in_=mirrored[:].rearrange("w b k q -> w b q k"),
             )
 
         xn_grouped = {}
@@ -339,6 +342,7 @@ def tile_dynamicgraphspatialconv_pa_kernel(tc, x, adj_param, w_cheb0, w_cheb1, o
             turn_row(slot, UPPER, banks)
         for slot in UPPER:
             add(banks[slot], slot, R)
+        regroup_weights()
         banks = [bank(k) for k in range(PACK)]
         for slot in LOWER:
             sigmoid(slot, R)
@@ -356,7 +360,7 @@ def tile_dynamicgraphspatialconv_pa_kernel(tc, x, adj_param, w_cheb0, w_cheb1, o
             add(banks[slot - PACK], slot, R)
         late = keep.tile([P, 2 * SLOTS * NODES], BF16, name="late", tag="sig", align_bytes=64)
         XC = T * QUARTER * PACK
-        for i, h in enumerate((3, 0, 1)):
+        for i, h in enumerate((0, 1)):
             xc_grouped[h] = late[:, i * XC : (i + 1) * XC].rearrange("p (t n j) -> p t n j", t=T, j=PACK)
         SG = 2 * QUARTER * PACK
         for h in range(2):
@@ -378,6 +382,8 @@ def tile_dynamicgraphspatialconv_pa_kernel(tc, x, adj_param, w_cheb0, w_cheb1, o
             x_turn_step(i)
         nc.vector.tensor_reduce(out=deg[:], in_=deg_parts[:], op=ALU.add, axis=AX.X)
         nc.vector.reciprocal(out=inv_deg[:], in_=deg[:])
+        quantise_weights()
+        regroup_x(vector_copy, 3, 0)
         x_group_step(0)
         nc.scalar.activation(out=inv_root[:], in_=inv_deg[:], func=ACT.Sqrt)
         factors = {R: bank(3)}
@@ -394,9 +400,11 @@ def tile_dynamicgraphspatialconv_pa_kernel(tc, x, adj_param, w_cheb0, w_cheb1, o
         quantise_x(0, 0)
         scale_columns(1, 2)
         quantise_x(0, 1)
+        factors[L] = bank(2)
+        spread(L, factors[L])
         for i in range(9, 12):
             x_group_step(i)
-        regroup_x(nc.scalar.copy, 3, 0)
+        regroup_x(nc.scalar.copy, 3, 1)
         quantise_s(2)
         quantise_x(1, 0)
         quantise_x(1, 1)
@@ -411,9 +419,8 @@ def tile_dynamicgraphspatialconv_pa_kernel(tc, x, adj_param, w_cheb0, w_cheb1, o
             lambda: scale_columns(0, 3),
             lambda: quantise_x(1, 2),
             lambda: scale_columns(1, 3),
-            regroup_weights,
             lambda: quantise_s(3),
-            lambda: (quantise_weights(), left_rows()),
+            left_rows,
             lambda: quantise_channels(3, 0, 2),
             lambda: scale_columns(0, 0),
             lambda: scale_columns(0, 1),
@@ -431,35 +438,29 @@ def tile_dynamicgraphspatialconv_pa_kernel(tc, x, adj_param, w_cheb0, w_cheb1, o
             lambda: quantise_channels(1, 0, 2),
             lambda: quantise_channels(1, 2, 3),
         ]
-        POPS = ((2, 1, 2, 1, 1, 1), (1, 1, 1, 1, 1, 1), (1, 1, 1, 1, 1, 1), (2, 1, 0, 0, 0, 0))
-        MIRRORS = ((0, 4), (0, 5), (1, 0), (1, 1))
-        tx_numbers = [1, 2, 4, 5]
+        MIRRORS = ((0, 4), (1, 0))
+        tx_numbers = [1, 4, 5, 0]
         both_numbers = [6, 7]
-        count = mirrors = 0
+        count = 0
         for i, h in enumerate(pairs):
             last = i == len(pairs) - 1
             order = [(b, t) for b in range(2) for t in range(T)] if last else [(b, t) for t in range(T) for b in range(2)]
             for step, (b, t) in enumerate(order):
                 tx1(2 * h + b, t, bank(tx_numbers[count % 4]))
                 count += 1
-                if i == 0 and step == 2:
-                    factors[L] = bank(0)
-                    spread(L, factors[L])
-                if i == 0 and step in (1, 3):
-                    regroup_x(nc.scalar.copy, 3, step // 2 + 1)
+                if i == 0 and step == 1:
+                    regroup_x(nc.scalar.copy, 3, 2)
                 if (i, step) in MIRRORS:
-                    k = mirrors
-                    mirror(k, bank(6 + k % 2, (P, PACK, P), BF16))
-                    mirrors += 1
-                for k in range(POPS[i][step]):
+                    mirror(i, bank(6 + i, (P, 2, PACK, P), BF16))
+                for k in range(2 if count <= 2 else 1):
                     if beside:
                         beside.pop(0)()
                 if last:
                     quantise_tx(h, t, block_of(b))
                 elif b == 1:
                     quantise_tx(h, t, slice(0, QUARTER))
-                if i > 0 and step in ((4, 5) if last else (3, 5)):
-                    k = step - 4 if last else step // 4
+                if i > 0 and step >= 4:
+                    k = step - 4
                     result(2 * pairs[i - 1] + k, bank(both_numbers[k], (P, T, C_OUT)))
         result(2 * pairs[-1], bank(both_numbers[0], (P, T, C_OUT)))
         both = bank(both_numbers[1], (P, T, C_OUT))

from contextlib import ExitStack

import concourse.mybir as mybir
from concourse.masks import make_identity

F32 = mybir.dt.float32
BF16 = mybir.dt.bfloat16
U32 = mybir.dt.uint32
U8 = mybir.dt.uint8
FP8X4 = mybir.dt.float8_e4m3fn_x4
ACT = mybir.ActivationFunctionType
ALU = mybir.AluOpType
AX = mybir.AxisListType

P = 128
PACK = 4
NODES = 1024
C_IN = 512
C_OUT = 128
T = 3
SLOTS = NODES // P
HALF = NODES // 2
QUARTERS = 4
QUARTER = NODES // QUARTERS
L, R = 0, 1
UPPER, LOWER = range(PACK), range(PACK, SLOTS)

FLOPS = 2 * NODES * NODES * T * C_IN + 2 * 2 * T * NODES * C_IN * C_OUT


def tile_dynamicgraphspatialconv_pa_kernel(tc, x, adj_param, w_cheb0, w_cheb1, out):
    nc = tc.nc
    with ExitStack() as stack:
        keep = stack.enter_context(tc.tile_pool(name="keep", bufs=1))
        stage = stack.enter_context(tc.tile_pool(name="stage", bufs=2))
        psum = stack.enter_context(tc.psum_pool(name="psum", bufs=1))
        stack.enter_context(tc.manual_schedule())

        adj_rows = adj_param.rearrange("(k c q) m -> c k q m", k=PACK, c=2)
        adj_sb = [keep.tile([P, 2, NODES], BF16, name="adj%d" % i, tag="adj%d" % i, align_bytes=64) for i in range(PACK)]

        def adj_of(slot):
            return adj_sb[slot // 2][:, slot % 2]

        x_rows = x[0].rearrange("(p j) (k c n) t -> c k p j (n t)", j=PACK, k=PACK, c=2)
        x_raw = [keep.tile([P, PACK, QUARTER * T], BF16, name="xraw%d" % h) for h in range(QUARTERS)]

        def load_x(slot):
            cols = slice((slot % 2) * P * T, (slot % 2 + 1) * P * T)
            nc.sync.dma_start(out=x_raw[slot // 2][:, :, cols], in_=x_rows[slot // PACK][slot % PACK])

        for half in range(2):
            cols = slice(half * HALF, (half + 1) * HALF)
            nc.sync.dma_start(out=adj_of(0)[:, cols], in_=adj_rows[0][0][:, cols])
        for slot in range(1, SLOTS):
            nc.sync.dma_start(out=adj_of(slot), in_=adj_rows[slot // PACK][slot % PACK])
            if slot in (1, 2):
                load_x(PACK + slot - 1)
        for slot in (6, 7):
            load_x(slot)
        w_raw = keep.tile([P, 2, PACK, C_OUT], BF16)
        nc.sync.dma_start(out=w_raw[:, 0], in_=w_cheb0.rearrange("(p j) o -> p j o", j=PACK))
        nc.sync.dma_start(out=w_raw[:, 1], in_=w_cheb1.rearrange("(j p) o -> p j o", j=PACK))
        x_turn_rows = x[0].rearrange("(j G e) (k n) t -> j (e k) G (n t)", j=PACK, G=PACK, k=PACK)
        x_turn = [keep.tile([P, PACK, QUARTER * T], BF16, name="xturn%d" % j) for j in range(PACK)]
        for j in range(PACK):
            nc.sync.dma_start(out=x_turn[j][:], in_=x_turn_rows[j])
        for slot in range(PACK):
            load_x(slot)

        ident = keep.tile([P, P], F32)
        make_identity(nc, ident[:])
        ident_bf = keep.tile([P, P], BF16)
        make_identity(nc, ident_bf[:])
        minus_diagonal = keep.tile([P, P], BF16)
        nc.vector.tensor_scalar(out=minus_diagonal[:], in0=ident_bf[:], scalar1=-16384.0, scalar2=None, op0=ALU.mult)
        deg_parts = keep.tile([P, SLOTS, 3], F32)
        nc.vector.memset(deg_parts[:], 0.0)

        sig = keep.tile([P, SLOTS, NODES], F32, name="sig", tag="sig", align_bytes=64)
        sym_right = keep.tile([P, SLOTS, HALF], F32)
        sym_left = keep.tile([P, PACK, HALF], F32)
        xn_codes = keep.tile([P, T, PACK, 2, P], U32, align_bytes=64)
        xn_scales = keep.tile([P, T, PACK, 2, P], U8, align_bytes=64)
        xc_codes = keep.tile([P, QUARTERS, T, QUARTER], U32, align_bytes=64)
        xc_scales = keep.tile([P, QUARTERS, T, QUARTER], U8, align_bytes=64)
        s_codes = keep.tile([P, QUARTERS, 2, QUARTER], U32, align_bytes=64)
        s_scales = keep.tile([P, QUARTERS, 2, QUARTER], U8, align_bytes=64)
        tx_codes = keep.tile([P, QUARTERS, T, QUARTER], U32, align_bytes=64)
        tx_scales = keep.tile([P, QUARTERS, T, QUARTER], U8, align_bytes=64)
        s_grouped = {h: keep.tile([P, 2, QUARTER, PACK], BF16, name="s%d" % h, align_bytes=64) for h in (2, 3)}
        inv_root = keep.tile([P, SLOTS], F32)
        deg = keep.tile([P, SLOTS], F32)
        inv_deg = keep.tile([P, SLOTS], F32)
        w_grouped = keep.tile([P, 2, C_OUT, PACK], BF16, align_bytes=64)
        w_codes = keep.tile([P, 2, C_OUT], U32, align_bytes=64)
        w_scales = keep.tile([P, 2, C_OUT], U8, align_bytes=64)
        out_rows = out[0].rearrange("t (k c q) o -> c k q t o", k=PACK, c=2)

        xc_early = keep.tile([P, T, QUARTER, PACK], BF16, align_bytes=64)
        xc_grouped = {2: xc_early, 3: xc_early}

        def bank(number, shape=(P, PACK, P), dtype=F32):
            return psum.tile(list(shape), dtype, name="bank%d" % number, tag="bank%d" % number)

        def columns(half):
            return slice(half * HALF, (half + 1) * HALF)

        def quarter(h):
            return slice(h * QUARTER, (h + 1) * QUARTER)

        def block_of(b):
            return slice(b * P, (b + 1) * P)

        def sigmoid(slot, half):
            nc.scalar.activation(
                out=sig[:, slot, columns(half)].rearrange("q (k w) -> q k w", k=PACK),
                in_=adj_of(slot).rearrange("q (k c w) -> q c k w", k=PACK, c=2)[:, half],
                func=ACT.Sigmoid,
                accum_out=(deg_parts[:, slot, 0:1] if (slot in LOWER and half == L) else None),
            )

        def first_sigmoids():
            for halves, blocks in ((slice(R, R + 1), slice(0, 2)), (slice(L, L + 1), slice(0, 2)), (slice(L, R + 1), slice(2, 4))):
                nc.scalar.activation(
                    out=sig[:, 0].rearrange("q (c k w) -> q c k w", c=2, k=PACK)[:, halves, blocks],
                    in_=adj_of(0).rearrange("q (k c w) -> q c k w", k=PACK, c=2)[:, halves, blocks],
                    func=ACT.Sigmoid,
                )

        def mask_diagonal(slots):
            first = slots[0]
            blocks = adj_sb[first // 2][:].rearrange("q s (b w) -> q (s b) w", w=P)
            start = 8 * (first % 2) + 2 * (first % PACK) + first // PACK
            diagonal = blocks[:, start : start + 10 * len(slots) - 9 : 10]
            nc.vector.tensor_tensor(
                out=diagonal,
                in0=diagonal,
                in1=minus_diagonal[:].unsqueeze(1).to_broadcast([P, len(slots), P]),
                op=ALU.add,
            )

        def turn_row(slot, column_slots, banks):
            for turned, column_slot in zip(banks, column_slots):
                nc.tensor.transpose(turned[:, slot % PACK, :], sig[:, slot, block_of(column_slot)], ident[:])

        def add(turned, slot, half):
            rows = sym_left if half == L else sym_right
            column = 0 if half == L else 1
            nc.vector.scalar_tensor_tensor(
                out=rows[:, slot],
                in0=turned[:].rearrange("q k w -> q (k w)"),
                scalar=1.0,
                in1=sig[:, slot, columns(half)],
                op0=ALU.mult,
                op1=ALU.add,
                accum_out=deg_parts[:, slot, column : column + 1],
            )

        def turn_adjacency(k, turned):
            for slot in UPPER:
                nc.tensor.transpose(turned[:, k % 2, slot, :], adj_of(slot)[:, block_of(2 * k + 1)], ident_bf[:])

        def add_column_sums(i, turned):
            for k in range(2):
                unused = stage.tile([P, HALF], F32, name="unused")
                nc.scalar.activation(
                    out=unused[:],
                    in_=turned[:, k].rearrange("q s w -> q (s w)"),
                    func=ACT.Sigmoid,
                    accum_out=deg_parts[:, PACK + 2 * i + k, 2:3],
                )

        def spread(half, along_free):
            for k in range(PACK):
                slot = half * PACK + k
                nc.tensor.transpose(along_free[:, k, :], inv_root[:, slot : slot + 1].to_broadcast([P, P]), ident[:])

        def scale_rows(engine, rows, slot, cols):
            engine.tensor_scalar(
                out=rows[:, slot, cols],
                in0=rows[:, slot, cols],
                scalar1=inv_root[:, slot : slot + 1],
                scalar2=-1.0,
                op0=ALU.mult,
                op1=ALU.mult,
            )

        def scale_columns(g, h):
            rows = sym_left if h < 2 else sym_right
            part = h % 2
            nc.vector.tensor_tensor(
                out=s_grouped[h][:, g],
                in0=rows[:, g * PACK : (g + 1) * PACK, quarter(part)].rearrange("q v w -> q w v"),
                in1=factors[h // 2][:, 2 * part : 2 * part + 2, :]
                .rearrange("q k w -> q (k w)")
                .unsqueeze(2)
                .to_broadcast([P, QUARTER, PACK]),
                op=ALU.mult,
            )

        def quantise_s(h):
            nc.vector.quantize_mx(
                out=s_codes[:, h].rearrange("q g w -> q (g w)").bitcast(FP8X4),
                scales=s_scales[:, h].rearrange("q g w -> q (g w)"),
                in_=s_grouped[h][:].rearrange("q g w v -> q (g w v)"),
            )

        def mirror(h, mirrored):
            for b in range(2):
                for k in range(PACK):
                    upper = s_grouped[2 + k // 2][:, 0, (k % 2) * P : (k % 2 + 1) * P, 2 * h + b]
                    nc.tensor.transpose(mirrored[:, b, k, :], upper, ident_bf[:])
            nc.scalar.copy(
                out=s_grouped[h][:, 1].rearrange("w (b q) k -> w b q k", b=2),
                in_=mirrored[:].rearrange("w b k q -> w b q k"),
            )

        xn_grouped = {}

        def turn_x(j, t, turned):
            for i in range(2 * PACK):
                g, G = i // PACK, i % PACK
                block = x_turn[j][:, G, :].rearrange("p (g n t) -> p g t n", g=2, t=T)[:, g, t, :]
                if i % 2 == 0:
                    nc.tensor.matmul(turned[:, i, :], lhsT=block, rhs=ident_bf[:], start=True, stop=True)
                else:
                    nc.tensor.transpose(turned[:, i, :], block, ident_bf[:])

        def group_x(j, t, turned):
            if j % 2 == 0:
                i = 3 * (j // 2) + t
                tag = "adj%d" % i if i < PACK else "xn%d" % i
                xn_grouped[j // 2, t] = keep.tile([P, 2, 2, P, PACK], BF16, name="xn%d" % i, tag=tag, align_bytes=64)
            nc.scalar.copy(
                out=xn_grouped[j // 2, t][:, j % 2].rearrange("q g c v -> q (g c v)").bitcast(F32),
                in_=turned[:].rearrange("q i c -> q (i c)").bitcast(F32),
            )

        def quantise_x(pair, t):
            js = slice(2 * pair, 2 * pair + 2)
            nc.vector.quantize_mx(
                out=xn_codes[:, t, js].rearrange("q j g p -> q (j g p)").bitcast(FP8X4),
                scales=xn_scales[:, t, js].rearrange("q j g p -> q (j g p)"),
                in_=xn_grouped[pair, t][:].rearrange("q j g p v -> q (j g p v)"),
            )

        def regroup_x(engine_copy, h, t, nodes=slice(0, QUARTER)):
            engine_copy(
                out=xc_grouped[h][:, t, nodes].rearrange("p (c i) j -> p c j i", i=PACK),
                in_=x_raw[h][:].rearrange("p j (c i t) -> p t c j i", i=PACK, t=T)[:, t, nodes.start // PACK : nodes.stop // PACK],
            )

        def quantise_channels(h, first, last):
            nc.vector.quantize_mx(
                out=xc_codes[:, h, first:last].rearrange("p t n -> p (t n)").bitcast(FP8X4),
                scales=xc_scales[:, h, first:last].rearrange("p t n -> p (t n)"),
                in_=xc_grouped[h][:, first:last].rearrange("p t n j -> p (t n j)"),
            )

        def regroup_weights():
            nc.vector.tensor_copy(out=w_grouped[:], in_=w_raw[:].rearrange("p k j o -> p k o j"))

        def quantise_weights():
            nc.vector.quantize_mx(
                out=w_codes[:].rearrange("p k o -> p (k o)").bitcast(FP8X4),
                scales=w_scales[:].rearrange("p k o -> p (k o)"),
                in_=w_grouped[:].rearrange("p k o j -> p (k o j)"),
            )

        tx_grouped = {}

        def tx1(b, t, tx):
            for j in range(PACK):
                for g in range(2):
                    nc.tensor.matmul_mx(
                        out=tx[:, j, :],
                        lhsT=xn_codes[:, t, j, g, :].bitcast(FP8X4),
                        lhsT_scale=xn_scales[:, t, j, g, :],
                        rhs=s_codes[:, b // 2, g, block_of(b % 2)].bitcast(FP8X4),
                        rhs_scale=s_scales[:, b // 2, g, block_of(b % 2)],
                        start=(g == 0),
                        stop=(g == 1),
                    )
            if b // 2 not in tx_grouped:
                tx_grouped[b // 2] = stage.tile([P, T, 2 * P, PACK], BF16, name="tx_grouped", align_bytes=64)
            nc.scalar.copy(
                out=tx_grouped[b // 2][:, t, block_of(b % 2), :], in_=tx[:].rearrange("p j v -> p v j")
            )

        def quantise_tx(h, t, part):
            nc.vector.quantize_mx(
                out=tx_codes[:, h, t, part].bitcast(FP8X4),
                scales=tx_scales[:, h, t, part],
                in_=tx_grouped[h][:, t, part].rearrange("p v j -> p (v j)"),
            )

        def result(b, both, steps=range(T)):
            for t in steps:
                for k, codes, scales in ((0, xc_codes, xc_scales), (1, tx_codes, tx_scales)):
                    nc.tensor.matmul_mx(
                        out=both[:, t, :],
                        lhsT=codes[:, b // 2, t, block_of(b % 2)].bitcast(FP8X4),
                        lhsT_scale=scales[:, b // 2, t, block_of(b % 2)],
                        rhs=w_codes[:, k, :].bitcast(FP8X4),
                        rhs_scale=w_scales[:, k, :],
                        start=(k == 0),
                        stop=(k == 1),
                    )
            part = slice(steps.start, steps.stop)
            rows = stage.tile([P, T, C_OUT], F32, name="rows", bufs=5)
            nc.scalar.copy(out=rows[:, part], in_=both[:, part])
            nc.sync.dma_start(out=out_rows[b // PACK][b % PACK][:, part], in_=rows[:, part])

        vector_copy = nc.vector.tensor_copy
        mask_diagonal((0,))
        mask_diagonal((1,))
        for part in range(2):
            for t in range(T):
                regroup_x(vector_copy, 2, t, block_of(part))
                if t == part:
                    mask_diagonal((2 + part,))
        quantise_channels(2, 0, 2)
        mask_diagonal((PACK, PACK + 1))
        quantise_channels(2, 2, 3)
        turned_adjacency = {}
        banks = [bank(k) for k in range(PACK)]
        for slot in UPPER:
            if slot == 0:
                first_sigmoids()
            else:
                sigmoid(slot, R)
                sigmoid(slot, L)
            turn_row(slot, UPPER, banks)
        for slot in UPPER:
            add(banks[slot], slot, L)
            if slot == 0:
                mask_diagonal((PACK + 2, PACK + 3))
        banks = [bank(PACK + k) for k in range(PACK)]
        for slot in LOWER:
            sigmoid(slot, L)
            turn_row(slot, UPPER, banks)
        for slot in UPPER:
            add(banks[slot], slot, R)
        regroup_weights()
        banks = [bank(k) for k in range(PACK)]
        for slot in LOWER:
            sigmoid(slot, R)
            turn_row(slot, LOWER, banks)
            if slot in (PACK + 1, PACK + 2):
                i = slot - PACK - 1
                turned_adjacency[i] = bank(PACK + i, (P, 2, PACK, P), BF16)
                for k in (2 * i, 2 * i + 1):
                    turn_adjacency(k, turned_adjacency[i])
        for i in range(2):
            add_column_sums(i, turned_adjacency[i])
        root_table = keep.tile([P, 1], F32)
        nc.scalar.activation(out=root_table[:], in_=ident[:, 0:1], func=ACT.Sqrt)
        for slot in LOWER:
            add(banks[slot - PACK], slot, R)
        late = keep.tile([P, 2 * SLOTS * NODES], BF16, name="late", tag="sig", align_bytes=64)
        XC = T * QUARTER * PACK
        for i, h in enumerate((0, 1)):
            xc_grouped[h] = late[:, i * XC : (i + 1) * XC].rearrange("p (t n j) -> p t n j", t=T, j=PACK)
        SG = 2 * QUARTER * PACK
        for h in range(2):
            first = 3 * XC + h * SG
            s_grouped[h] = late[:, first : first + SG].rearrange("p (g w v) -> p g w v", g=2, v=PACK)

        steps = [(j, t) for j in range(PACK) for t in range(T)]
        x_numbers = [6, 7, 4, 5, 0, 1, 2, 6, 7, 4, 5, 0]
        x_banks = {}

        def x_turn_step(i):
            x_banks[i] = bank(x_numbers[i], (P, SLOTS, P), BF16)
            turn_x(*steps[i], x_banks[i])

        def x_group_step(i):
            group_x(*steps[i], x_banks[i])

        for i in range(6):
            x_turn_step(i)
        nc.vector.tensor_reduce(out=deg[:], in_=deg_parts[:], op=ALU.add, axis=AX.X)
        nc.vector.reciprocal(out=inv_deg[:], in_=deg[:])
        quantise_weights()
        regroup_x(vector_copy, 3, 0)
        x_group_step(0)
        nc.scalar.activation(out=inv_root[:], in_=inv_deg[:], func=ACT.Sqrt)
        factors = {R: bank(3)}
        spread(R, factors[R])
        x_turn_step(6)
        for i in range(1, 4):
            x_group_step(i)
        for v in range(SLOTS):
            scale_rows(nc.vector, sym_right, v, slice(0, HALF))
        for i in range(7, 12):
            x_turn_step(i)
            x_group_step(i - 3)
        scale_columns(0, 2)
        quantise_x(0, 0)
        scale_columns(1, 2)
        quantise_x(0, 1)
        factors[L] = bank(2)
        spread(L, factors[L])
        for i in range(9, 12):
            x_group_step(i)
        regroup_x(nc.scalar.copy, 3, 1)
        quantise_s(2)
        quantise_x(1, 0)
        quantise_x(1, 1)

        pairs = (2, 3, 0, 1)
        def left_rows():
            for v in UPPER:
                scale_rows(nc.vector, sym_left, v, slice(0, HALF))

        beside = [
            lambda: quantise_x(0, 2),
            lambda: scale_columns(0, 3),
            lambda: quantise_x(1, 2),
            lambda: scale_columns(1, 3),
            lambda: quantise_s(3),
            left_rows,
            lambda: quantise_channels(3, 0, 2),
            lambda: scale_columns(0, 0),
            lambda: scale_columns(0, 1),
            lambda: quantise_s(0),
            lambda: quantise_channels(3, 2, 3),
            lambda: quantise_s(1),
            lambda: regroup_x(vector_copy, 0, 0),
            lambda: regroup_x(vector_copy, 0, 1),
            lambda: regroup_x(vector_copy, 0, 2),
            lambda: quantise_channels(0, 0, 2),
            lambda: quantise_channels(0, 2, 3),
            lambda: regroup_x(vector_copy, 1, 0),
            lambda: regroup_x(vector_copy, 1, 1),
            lambda: regroup_x(vector_copy, 1, 2),
            lambda: quantise_channels(1, 0, 2),
            lambda: quantise_channels(1, 2, 3),
        ]
        MIRRORS = ((0, 4), (1, 0))
        tx_numbers = [1, 4, 5, 0]
        both_numbers = [6, 7]
        count = 0
        for i, h in enumerate(pairs):
            last = i == len(pairs) - 1
            order = [(b, t) for b in range(2) for t in range(T)] if last else [(b, t) for t in range(T) for b in range(2)]
            for step, (b, t) in enumerate(order):
                tx1(2 * h + b, t, bank(tx_numbers[count % 4]))
                count += 1
                if i == 0 and step == 1:
                    regroup_x(nc.scalar.copy, 3, 2)
                if (i, step) in MIRRORS:
                    mirror(i, bank(6 + i, (P, 2, PACK, P), BF16))
                for k in range(2 if count <= 2 else 1):
                    if beside:
                        beside.pop(0)()
                if last:
                    quantise_tx(h, t, block_of(b))
                elif b == 1:
                    quantise_tx(h, t, slice(0, QUARTER))
                if i > 0 and step >= 4:
                    k = step - 4
                    result(2 * pairs[i - 1] + k, bank(both_numbers[k], (P, T, C_OUT)))
        result(2 * pairs[-1], bank(both_numbers[0], (P, T, C_OUT)))
        both = bank(both_numbers[1], (P, T, C_OUT))
        result(2 * pairs[-1] + 1, both, range(2))
        result(2 * pairs[-1] + 1, both, range(2, T))
